import numpy as np
import ml_dtypes


def mxq(x, axis, fmt="e4m3"):
    dtype, down = {"e4m3": (ml_dtypes.float8_e4m3fn, 7), "e5m2": (ml_dtypes.float8_e5m2, 14)}[fmt]
    v = np.moveaxis(np.asarray(x, np.float32).astype(ml_dtypes.bfloat16).astype(np.float64), axis, -1)
    blocks = v.reshape(v.shape[:-1] + (-1, 32))
    amax = np.abs(blocks).max(-1, keepdims=True)
    byte = np.maximum(np.where(amax > 0, np.frexp(amax)[1] - 1 + 127, 0) - down, 1)
    scale = np.exp2(byte - 127.0)
    codes = (blocks / scale).astype(np.float32).astype(dtype).astype(np.float64)
    return np.moveaxis((codes * scale).reshape(v.shape), -1, axis)


WIDE = False


def mx_kscale(k):
    if not WIDE:
        return np.ones(k)
    levels = np.array([10, -10, 5, -5, 0])
    a = np.random.permutation(np.resize(levels, k // 512 * 4)).reshape(k // 512, 4)
    idx = np.arange(k)
    return np.exp2(a[idx // 512, idx % 128 // 32])


BF16 = ml_dtypes.bfloat16


def bf(x):
    return np.asarray(x, np.float32).astype(BF16)


def f64(x):
    return np.asarray(x).astype(np.float64)


S, B, ND, NS, HN, BT, C, Hd, Wd = 8, 1024, 32, 96, 512, 512, 2, 16, 16
P = C * Hd * Wd
EPS = 1e-9
SELU_ALPHA = 1.6732632423543772848170429916717
SELU_SCALE = 1.0507009873554804934193349852946


def selu(v):
    return SELU_SCALE * np.where(v > 0, v, SELU_ALPHA * np.expm1(np.minimum(v, 0.0)))


def sigmoid(v):
    return 1.0 / (1.0 + np.exp(-v))


def grid(v, bits):
    return np.round(v * np.exp2(bits)) / np.exp2(bits)


def setup_inputs():
    t = mx_kscale(HN)
    return {"digits": bf(grid(np.random.random_sample((S, B, ND)), 7)),
            "styles": bf(grid(np.random.standard_normal((S, B, NS)), 5)),
            "images": bf(np.random.random_sample((S, B, C, Hd, Wd))),
            "W_h": bf(grid(np.random.standard_normal((ND + NS, HN)) / np.sqrt(ND + NS), 10) * t),
            "b_h": bf(grid(np.random.standard_normal(HN) * 0.5, 7) * t),
            "W1": bf(np.random.standard_normal((HN, BT)) * 1.4 / np.sqrt(HN) / t[:, None]),
            "b1": bf(np.random.standard_normal(BT) * 0.5),
            "W2": bf(np.random.standard_normal((BT, P)) / np.sqrt(BT)),
            "b2": bf(np.random.standard_normal(P) * 0.5)}


def reference(digits, styles, images, W_h, b_h, W1, b1, W2, b2):
    h = np.maximum(np.concatenate([f64(digits), f64(styles)], axis=-1) @ f64(W_h) + f64(b_h), 0.0)
    t = selu((mxq(h, 2, "e4m3") @ mxq(f64(W1), 0, "e4m3")) + f64(b1))
    x_hat = sigmoid((mxq(t, 2, "e4m3") @ mxq(f64(W2), 0, "e4m3")) + f64(b2))
    images_mean = x_hat.reshape(x_hat.shape[0], x_hat.shape[1], C, Hd, Wd)
    img = f64(images)
    loss = -(np.log(images_mean + EPS) * img + np.log(1.0 - images_mean + EPS) * (1.0 - img)).sum(-1)
    return loss

@@ -1,0 +1,360 @@
+from contextlib import ExitStack
+import math
+
+import concourse.bass as bass
+import concourse.mybir as mybir
+import concourse.tile as tile
+from concourse.masks import make_identity
+
+F32 = mybir.dt.float32
+BF16 = mybir.dt.bfloat16
+U32 = mybir.dt.uint32
+U8 = mybir.dt.uint8
+FP8X4 = mybir.dt.float8_e4m3fn_x4
+ALU = mybir.AluOpType
+ACTF = mybir.ActivationFunctionType
+AX = mybir.AxisListType
+
+P = 128
+NB = 64
+NT = 16
+CH = 4
+NCH = 4
+FLOPS = 2 * 8192 * (128 * 512 + 2 * 512 * 512)
+
+ALPHA = 1.6732632423543772848170429916717
+SCALE = 1.0507009873554804934193349852946
+SA = SCALE * ALPHA
+LN_SA = math.log(SA)
+EPS = 1e-9
+DMAX = math.log((1.0 + EPS) / EPS)
+
+
+def tile_decoder_t_kernel(tc, digits, styles, images, W_h, b_h, W1, b1, W2, b2, out):
+    nc = tc.nc
+    dig = digits.rearrange("s b d -> (s b) d").rearrange("(p n) d -> p n d", n=NB)
+    sty = styles.rearrange("s b d -> (s b) d").rearrange("(p n) d -> p n d", n=NB)
+    imgv = images.rearrange("s b c h w -> (s b) (c h w)").rearrange("(p n) x -> p n x", n=NB)
+    outv = out.rearrange("s b c h -> (s b) (c h)").rearrange("(p n) g -> p n g", n=NB)
+
+    with ExitStack() as ctx:
+        ctx.enter_context(tc.manual_schedule())
+        const = ctx.enter_context(tc.tile_pool(name="const", bufs=1))
+        work = ctx.enter_context(tc.tile_pool(name="work", bufs=2))
+        pmm = ctx.enter_context(tc.psum_pool(name="pmm", bufs=3))
+        pl0 = ctx.enter_context(tc.psum_pool(name="pl0", bufs=2))
+        pim = ctx.enter_context(tc.psum_pool(name="pim", bufs=2))
+        pacc = ctx.enter_context(tc.psum_pool(name="pacc", bufs=1))
+
+        cat = {}
+        catT = {}
+        hg = {}
+        hq = {}
+        hs = {}
+        ee = {}
+        rr = {}
+        tq = {}
+        ts = {}
+        xx = {}
+        aa = {}
+        bb = {}
+        img = {}
+        im1 = {}
+        acc = {}
+
+        idb = const.tile([P, P], BF16, name="idb")
+        idf = const.tile([P, P], F32, name="idf")
+        make_identity(nc, idb[:])
+        make_identity(nc, idf[:])
+        brow = const.tile([P, P], BF16, name="brow")
+        nc.vector.memset(brow[:], 0.0)
+        eps_t = const.tile([P, 1], F32, name="eps_t")
+        ope_t = const.tile([P, 1], F32, name="ope_t")
+        nc.vector.memset(eps_t[:], EPS)
+        nc.vector.tensor_scalar_add(out=ope_t[:], in0=eps_t[:], scalar1=1.0)
+
+        def ld_cat(c):
+            cat[c] = work.tile([P, 16, P], BF16, name="cat", tag="cat", bufs=2)
+            nc.sync.dma_start(out=cat[c][:, :, 0:32], in_=dig[:, 16 * c:16 * c + 16, :])
+            nc.sync.dma_start(out=cat[c][:, :, 32:128], in_=sty[:, 16 * c:16 * c + 16, :])
+
+        def ld_img(t):
+            img[t] = work.tile([P, 4, 512], BF16, name="img", tag="img", bufs=3)
+            nc.sync.dma_start(out=img[t][:], in_=imgv[:, 4 * t:4 * t + 4, :])
+
+        ld_cat(0)
+        wh = const.tile([P, 512], BF16, name="wh")
+        nc.sync.dma_start(out=wh[:], in_=W_h)
+        nc.sync.dma_start(out=brow[0:4, :], in_=b_h.rearrange("(j c) -> j c", j=4))
+        nc.sync.dma_start(out=brow[4:8, :], in_=b1.rearrange("(j c) -> j c", j=4))
+        nc.sync.dma_start(
+            out=brow[8:12, :].rearrange("m (g r) -> m g r", r=4),
+            in_=b2.rearrange("(g m r) -> m g r", m=4, r=4),
+        )
+        raw1 = work.tile([P, 4, 512], BF16, name="raw1", tag="raw", bufs=2)
+        nc.sync.dma_start(out=raw1[:], in_=W1.rearrange("(j p) n -> p j n", p=P))
+        raw2 = work.tile([P, 4, 512], BF16, name="raw2", tag="raw", bufs=2)
+        nc.sync.dma_start(out=raw2[:], in_=W2.rearrange("(j p) n -> p j n", p=P))
+        for t in range(3):
+            ld_img(t)
+
+        pb = pl0.tile([P, P], BF16, name="pb", tag="l0")
+        nc.tensor.transpose(pb[:], brow[:], idb[:])
+        bias = const.tile([P, 12], F32, name="bias")
+        nc.vector.tensor_copy(out=bias[:], in_=pb[:, 0:12])
+        b1e = const.tile([P, 4], F32, name="b1e")
+        sb1 = const.tile([P, 4], F32, name="sb1")
+        nc.vector.tensor_scalar_add(out=b1e[:], in0=bias[:, 4:8], scalar1=LN_SA)
+        nc.vector.tensor_scalar_mul(out=sb1[:], in0=bias[:, 4:8], scalar1=SCALE)
+        bh_bc = bias[:, 0:4].unsqueeze(1).to_broadcast([P, P, 4])
+
+        w1c = const.tile([P, 512], U32, name="w1c", align_bytes=64)
+        w1s = const.tile([P, 512], U8, name="w1s", align_bytes=64)
+        w2c = const.tile([P, 512], U32, name="w2c", align_bytes=64)
+        w2s = const.tile([P, 512], U8, name="w2s", align_bytes=64)
+        out_sb = const.tile([P, NB, 32], F32, name="out_sb")
+
+        def quant_w1():
+            grp = work.tile([P, 512, 4], BF16, name="grp1", tag="grp", bufs=1, align_bytes=64)
+            nc.vector.tensor_copy(
+                out=grp[:].rearrange("p (c i) j -> p c j i", i=4),
+                in_=raw1[:].rearrange("p j (c i) -> p c j i", i=4),
+            )
+            nc.vector.quantize_mx(
+                out=w1c[:].bitcast(FP8X4), scales=w1s[:], in_=grp[:].rearrange("p n j -> p (n j)")
+            )
+
+        def quant_w2():
+            grp = work.tile([P, 512, 4], BF16, name="grp2", tag="grp", bufs=1, align_bytes=64)
+            src = raw2[:].rearrange("p j (g m r) -> p m g j r", m=4, r=4)
+            for m in range(4):
+                nc.vector.tensor_copy(
+                    out=grp[:, m * P:(m + 1) * P, :].rearrange("p (g r) j -> p g j r", r=4),
+                    in_=src[:, m],
+                )
+            nc.vector.quantize_mx(
+                out=w2c[:].bitcast(FP8X4), scales=w2s[:], in_=grp[:].rearrange("p n j -> p (n j)")
+            )
+
+        def u0_a(t):
+            c = t // CH
+            ct = pl0.tile([P, 512], BF16, name="ct", tag="l0")
+            for s in range(4):
+                nc.tensor.transpose(ct[:, s * P:(s + 1) * P], cat[c][:, (t % CH) * 4 + s, :], idb[:])
+            catT[t] = work.tile([P, 512], BF16, name="catT", tag="catT", bufs=2)
+            nc.vector.tensor_copy(out=catT[t][:], in_=ct[:])
+            hg[t] = work.tile([P, 512, 4], BF16, name="hg", tag="hg", bufs=2, align_bytes=64)
+
+        def u0_b(t, s):
+            p0 = pl0.tile([P, 4, P], F32, name="p0", tag="l0")
+            for j in range(4):
+                nc.tensor.matmul(
+                    out=p0[:, j, :],
+                    lhsT=wh[:, j * P:(j + 1) * P],
+                    rhs=catT[t][:, s * P:(s + 1) * P],
+                    start=True,
+                    stop=True,
+                )
+            nc.vector.tensor_tensor(
+                out=hg[t][:, s * P:(s + 1) * P, :],
+                in0=p0[:].rearrange("p j w -> p w j"),
+                in1=bh_bc,
+                op=ALU.add,
+            )
+
+        def u0_c(t):
+            flat = hg[t][:].rearrange("p w j -> p (w j)")
+            nc.vector.tensor_scalar_max(out=flat, in0=flat, scalar1=0.0)
+            hq[t] = work.tile([P, 512], U32, name="hq", tag="hq", bufs=4, align_bytes=64)
+            hs[t] = work.tile([P, 512], U8, name="hs", tag="hs", bufs=4, align_bytes=64)
+            nc.vector.quantize_mx(out=hq[t][:].bitcast(FP8X4), scales=hs[t][:], in_=flat)
+
+        def u0_pieces(t):
+            return (
+                [lambda: u0_a(t)]
+                + [(lambda s: (lambda: u0_b(t, s)))(s) for s in range(4)]
+                + [lambda: u0_c(t)]
+            )
+
+        def m1(t, m):
+            if m == 0:
+                ee[t] = work.tile([P, 4, 512], F32, name="ee", tag="ee", bufs=2)
+                rr[t] = work.tile([P, 4, 512], BF16, name="rr", tag="rr", bufs=2)
+            p1 = pmm.tile([P, 512], F32, name="p1", tag="mm")
+            nc.tensor.matmul_mx(
+                out=p1[:],
+                lhsT=w1c[:, m * P:(m + 1) * P].bitcast(FP8X4),
+                lhsT_scale=w1s[:, m * P:(m + 1) * P],
+                rhs=hq[t][:].bitcast(FP8X4),
+                rhs_scale=hs[t][:],
+                start=True,
+                stop=True,
+            )
+            nc.scalar.activation(out=ee[t][:, m, :], in_=p1[:], func=ACTF.Exp, bias=b1e[:, m:m + 1], scale=1.0)
+            nc.scalar.activation(out=rr[t][:, m, :], in_=p1[:], func=ACTF.Relu, bias=sb1[:, m:m + 1], scale=SCALE)
+
+        def c1(t):
+            tpl = work.tile([P, 4, 512], BF16, name="tpl", tag="tpl", bufs=1)
+            nc.vector.scalar_tensor_tensor(
+                out=tpl[:].rearrange("p m w -> p (m w)"),
+                in0=ee[t][:].rearrange("p m w -> p (m w)"),
+                scalar=SA,
+                in1=rr[t][:].rearrange("p m w -> p (m w)"),
+                op0=ALU.subtract,
+                op1=ALU.min,
+            )
+            tg = work.tile([P, 512, 4], BF16, name="tg", tag="tg", bufs=2, align_bytes=64)
+            nc.vector.tensor_copy(
+                out=tg[:].rearrange("p (c i) j -> p c j i", i=4),
+                in_=tpl[:].rearrange("p j (c i) -> p c j i", i=4),
+            )
+            tq[t] = work.tile([P, 512], U32, name="tq", tag="tq", bufs=4, align_bytes=64)
+            ts[t] = work.tile([P, 512], U8, name="ts", tag="ts", bufs=4, align_bytes=64)
+            nc.vector.quantize_mx(
+                out=tq[t][:].bitcast(FP8X4), scales=ts[t][:], in_=tg[:].rearrange("p w j -> p (w j)")
+            )
+
+        def m2(t, m):
+            if m == 0:
+                xx[t] = work.tile([P, 4, 512], F32, name="xx", tag="xx", bufs=4)
+            p2 = pmm.tile([P, 512], F32, name="p2", tag="mm")
+            nc.tensor.matmul_mx(
+                out=p2[:],
+                lhsT=w2c[:, m * P:(m + 1) * P].bitcast(FP8X4),
+                lhsT_scale=w2s[:, m * P:(m + 1) * P],
+                rhs=tq[t][:].bitcast(FP8X4),
+                rhs_scale=ts[t][:],
+                start=True,
+                stop=True,
+            )
+            nc.scalar.activation(out=xx[t][:, m, :], in_=p2[:], func=ACTF.Sigmoid, bias=bias[:, 8 + m:9 + m], scale=1.0)
+
+        def ln(t):
+            aa[t] = work.tile([P, 4, 512], F32, name="aa", tag="aa", bufs=3)
+            bb[t] = work.tile([P, 4, 512], F32, name="bb", tag="bb", bufs=3)
+            xf = xx[t][:].rearrange("p m w -> p (m w)")
+            af = aa[t][:].rearrange("p m w -> p (m w)")
+            bf = bb[t][:].rearrange("p m w -> p (m w)")
+            nc.scalar.activation(out=af, in_=xf, func=ACTF.Ln, bias=eps_t[:], scale=1.0)
+            nc.scalar.activation(out=bf, in_=xf, func=ACTF.Ln, bias=ope_t[:], scale=-1.0)
+            nc.gpsimd.tensor_tensor(out=bf, in0=bf, in1=af, op=ALU.subtract)
+
+        def im(t):
+            im1[t] = work.tile([P, 4, 512], F32, name="im1", tag="im1", bufs=4)
+            for s in range(4):
+                nc.gpsimd.tensor_scalar(
+                    out=im1[t][:, s, :].rearrange("p (m g r) -> p m g r", m=4, r=4),
+                    in0=img[t][:, s, :].rearrange("p (g m r) -> p m g r", m=4, r=4),
+                    scalar1=-1.0,
+                    scalar2=1.0,
+                    op0=ALU.mult,
+                    op1=ALU.add,
+                )
+
+        def tk(t, m):
+            imT = pim.tile([P, 4, P], F32, name="imT", tag="im")
+            for s in range(4):
+                nc.tensor.transpose(imT[:, s, :], im1[t][:, s, m * P:(m + 1) * P], idf[:])
+            nc.vector.scalar_tensor_tensor(
+                out=bb[t][:, m, :],
+                in0=bb[t][:, m, :],
+                scalar=-DMAX,
+                in1=imT[:].rearrange("p s w -> p (s w)"),
+                op0=ALU.max,
+                op1=ALU.mult,
+            )
+
+        def ta(t, s):
+            if s == 0:
+                acc[t] = pacc.tile([P, 4, P], F32, name="acc", tag="acc")
+            for m in range(4):
+                nc.tensor.matmul(
+                    out=acc[t][:, s, :],
+                    lhsT=aa[t][:, m, s * P:(s + 1) * P],
+                    rhs=idf[:],
+                    is_transpose=True,
+                    start=(m == 0),
+                    stop=False,
+                )
+            for m in range(4):
+                nc.tensor.matmul(
+                    out=acc[t][:, s, :],
+                    lhsT=bb[t][:, m, s * P:(s + 1) * P],
+                    rhs=idf[:],
+                    is_transpose=True,
+                    start=False,
+                    stop=(m == 3),
+                )
+
+        def tr(t):
+            red = work.tile([P, P], F32, name="red", tag="red", bufs=2)
+            nc.vector.tensor_reduce(
+                out=red[:], in_=acc[t][:].rearrange("p s (g r) -> p (s g) r", r=4), axis=AX.X, op=ALU.add
+            )
+            nc.vector.tensor_scalar_mul(
+                out=out_sb[:, 4 * t:4 * t + 4, :].rearrange("p s g -> p (s g)"), in0=red[:], scalar1=-1.0
+            )
+            if t % CH == CH - 1:
+                c = t // CH
+                nc.sync.dma_start(out=outv[:, 16 * c:16 * c + 16, :], in_=out_sb[:, 16 * c:16 * c + 16, :])
+
+        def tail(t):
+            for m in range(4):
+                tk(t, m)
+            for s in range(4):
+                ta(t, s)
+            tr(t)
+
+        def run(pieces):
+            for f in pieces:
+                f()
+
+        run(u0_pieces(0))
+        quant_w1()
+        run(u0_pieces(1))
+        quant_w2()
+        for c in range(NCH):
+            b = c * CH
+            n = b + CH
+            last = c == NCH - 1
+            if not last:
+                ld_cat(c + 1)
+            for k in range(CH):
+                t = b + k
+                for m in range(4):
+                    m1(t, m)
+                    if c > 0 and k == 1:
+                        ta(b - 1, m)
+                if c == 0 and k < 2:
+                    run(u0_pieces(k + 2))
+                if c > 0 and k == 0:
+                    for m in range(4):
+                        tk(b - 1, m)
+                if c > 0 and k == 1:
+                    tr(b - 1)
+                c1(t)
+                im(t)
+                if t + 3 < NT:
+                    ld_img(t + 3)
+            fill = []
+            if not last:
+                fill = u0_pieces(n) + u0_pieces(n + 1)
+            used = 0
+            for i in range(4 * CH):
+                m2(b + i // 4, i % 4)
+                if i >= 3 and used < len(fill):
+                    fill[used]()
+                    used += 1
+            run(fill[used:])
+            ln(b)
+            if not last:
+                run(u0_pieces(n + 2))
+            ln(b + 1)
+            if not last:
+                run(u0_pieces(n + 3))
+            tail(b)
+            ln(b + 2)
+            tail(b + 1)
+            ln(b + 3)
+            tail(b + 2)
+        tail(NT - 1)

@@ -176,11 +176,23 @@ def tile_decoder_t_kernel(tc, digits, styles, images, W_h, b_h, W1, b1, W2, b2, 
                 + [lambda: u0_c(t)]
             )
 
+        def warm(bank):
+            nc.tensor.matmul_mx(
+                out=bank,
+                lhsT=w1c[:, 0:P].bitcast(FP8X4),
+                lhsT_scale=w1s[:, 0:P],
+                rhs=w1c[:].bitcast(FP8X4),
+                rhs_scale=w1s[:],
+                start=True,
+                stop=True,
+            )
+
         def m1(t, m):
             if m == 0:
                 ee[t] = work.tile([P, 4, 512], F32, name="ee", tag="ee", bufs=2)
                 rr[t] = work.tile([P, 4, 512], BF16, name="rr", tag="rr", bufs=2)
             p1 = pmm.tile([P, 512], F32, name="p1", tag="mm")
+            warm(p1[:])
             nc.tensor.matmul_mx(
                 out=p1[:],
                 lhsT=w1c[:, m * P:(m + 1) * P].bitcast(FP8X4),
@@ -253,6 +265,7 @@ def tile_decoder_t_kernel(tc, digits, styles, images, W_h, b_h, W1, b1, W2, b2, 
 
         def tk(t, m):
             imT = pim.tile([P, 4, P], F32, name="imT", tag="im")
+            warm(imT[:].rearrange("p s w -> p (s w)"))
             for s in range(4):
                 nc.tensor.transpose(imT[:, s, :], im1[t][:, s, m * P:(m + 1) * P], idf[:])
             nc.vector.scalar_tensor_tensor(
@@ -267,6 +280,7 @@ def tile_decoder_t_kernel(tc, digits, styles, images, W_h, b_h, W1, b1, W2, b2, 
         def ta(t, s):
             if s == 0:
                 acc[t] = pacc.tile([P, 4, P], F32, name="acc", tag="acc")
+                warm(acc[t][:].rearrange("p s w -> p (s w)"))
             for m in range(4):
                 nc.tensor.matmul(
                     out=acc[t][:, s, :],

@@ -20,6 +20,7 @@ NB = 64
 NT = 16
 CH = 4
 NCH = 4
+LA = 4
 FLOPS = 2 * 8192 * (128 * 512 + 2 * 512 * 512)
 
 ALPHA = 1.6732632423543772848170429916717
@@ -41,10 +42,8 @@ def tile_decoder_t_kernel(tc, digits, styles, images, W_h, b_h, W1, b1, W2, b2, 
         ctx.enter_context(tc.manual_schedule())
         const = ctx.enter_context(tc.tile_pool(name="const", bufs=1))
         work = ctx.enter_context(tc.tile_pool(name="work", bufs=2))
-        pmm = ctx.enter_context(tc.psum_pool(name="pmm", bufs=3))
-        pl0 = ctx.enter_context(tc.psum_pool(name="pl0", bufs=2))
-        pim = ctx.enter_context(tc.psum_pool(name="pim", bufs=2))
-        pacc = ctx.enter_context(tc.psum_pool(name="pacc", bufs=1))
+        pmm = ctx.enter_context(tc.psum_pool(name="pmm", bufs=LA))
+        psd = ctx.enter_context(tc.psum_pool(name="psd", bufs=8 - LA))
 
         cat = {}
         catT = {}
@@ -59,7 +58,8 @@ def tile_decoder_t_kernel(tc, digits, styles, images, W_h, b_h, W1, b1, W2, b2, 
         aa = {}
         bb = {}
         img = {}
-        im1 = {}
+        imp = {}
+        pp = {}
         acc = {}
 
         idb = const.tile([P, P], BF16, name="idb")
@@ -98,7 +98,7 @@ def tile_decoder_t_kernel(tc, digits, styles, images, W_h, b_h, W1, b1, W2, b2, 
         for t in range(3):
             ld_img(t)
 
-        pb = pl0.tile([P, P], BF16, name="pb", tag="l0")
+        pb = psd.tile([P, P], BF16, name="pb", tag="sd")
         nc.tensor.transpose(pb[:], brow[:], idb[:])
         bias = const.tile([P, 12], F32, name="bias")
         nc.vector.tensor_copy(out=bias[:], in_=pb[:, 0:12])
@@ -106,6 +106,8 @@ def tile_decoder_t_kernel(tc, digits, styles, images, W_h, b_h, W1, b1, W2, b2, 
         sb1 = const.tile([P, 4], F32, name="sb1")
         nc.vector.tensor_scalar_add(out=b1e[:], in0=bias[:, 4:8], scalar1=LN_SA)
         nc.vector.tensor_scalar_mul(out=sb1[:], in0=bias[:, 4:8], scalar1=SCALE)
+        nb2 = const.tile([P, 4], F32, name="nb2")
+        nc.vector.tensor_scalar_mul(out=nb2[:], in0=bias[:, 8:12], scalar1=-1.0)
         bh_bc = bias[:, 0:4].unsqueeze(1).to_broadcast([P, P, 4])
 
         w1c = const.tile([P, 512], U32, name="w1c", align_bytes=64)
@@ -114,31 +116,32 @@ def tile_decoder_t_kernel(tc, digits, styles, images, W_h, b_h, W1, b1, W2, b2, 
         w2s = const.tile([P, 512], U8, name="w2s", align_bytes=64)
         out_sb = const.tile([P, NB, 32], F32, name="out_sb")
 
-        def quant_w1():
-            grp = work.tile([P, 512, 4], BF16, name="grp1", tag="grp", bufs=1, align_bytes=64)
-            nc.vector.tensor_copy(
-                out=grp[:].rearrange("p (c i) j -> p c j i", i=4),
-                in_=raw1[:].rearrange("p j (c i) -> p c j i", i=4),
+        grp1 = work.tile([P, 512, 4], BF16, name="grp1", tag="grp", bufs=2, align_bytes=64)
+        nc.scalar.copy(
+            out=grp1[:].rearrange("p (c i) j -> p c j i", i=4),
+            in_=raw1[:].rearrange("p j (c i) -> p c j i", i=4),
+        )
+        grp2 = work.tile([P, 512, 4], BF16, name="grp2", tag="grp", bufs=2, align_bytes=64)
+        src2 = raw2[:].rearrange("p j (g m r) -> p m g j r", m=4, r=4)
+        for m in range(4):
+            nc.scalar.copy(
+                out=grp2[:, m * P:(m + 1) * P, :].rearrange("p (g r) j -> p g j r", r=4),
+                in_=src2[:, m],
             )
+
+        def quant_w1():
             nc.vector.quantize_mx(
-                out=w1c[:].bitcast(FP8X4), scales=w1s[:], in_=grp[:].rearrange("p n j -> p (n j)")
+                out=w1c[:].bitcast(FP8X4), scales=w1s[:], in_=grp1[:].rearrange("p n j -> p (n j)")
             )
 
         def quant_w2():
-            grp = work.tile([P, 512, 4], BF16, name="grp2", tag="grp", bufs=1, align_bytes=64)
-            src = raw2[:].rearrange("p j (g m r) -> p m g j r", m=4, r=4)
-            for m in range(4):
-                nc.vector.tensor_copy(
-                    out=grp[:, m * P:(m + 1) * P, :].rearrange("p (g r) j -> p g j r", r=4),
-                    in_=src[:, m],
-                )
             nc.vector.quantize_mx(
-                out=w2c[:].bitcast(FP8X4), scales=w2s[:], in_=grp[:].rearrange("p n j -> p (n j)")
+                out=w2c[:].bitcast(FP8X4), scales=w2s[:], in_=grp2[:].rearrange("p n j -> p (n j)")
             )
 
         def u0_a(t):
             c = t // CH
-            ct = pl0.tile([P, 512], BF16, name="ct", tag="l0")
+            ct = psd.tile([P, 512], BF16, name="ct", tag="sd")
             for s in range(4):
                 nc.tensor.transpose(ct[:, s * P:(s + 1) * P], cat[c][:, (t % CH) * 4 + s, :], idb[:])
             catT[t] = work.tile([P, 512], BF16, name="catT", tag="catT", bufs=2)
@@ -146,7 +149,7 @@ def tile_decoder_t_kernel(tc, digits, styles, images, W_h, b_h, W1, b1, W2, b2, 
             hg[t] = work.tile([P, 512, 4], BF16, name="hg", tag="hg", bufs=2, align_bytes=64)
 
         def u0_b(t, s):
-            p0 = pl0.tile([P, 4, P], F32, name="p0", tag="l0")
+            p0 = psd.tile([P, 4, P], F32, name="p0", tag="sd")
             for j in range(4):
                 nc.tensor.matmul(
                     out=p0[:, j, :],
@@ -176,34 +179,42 @@ def tile_decoder_t_kernel(tc, digits, styles, images, W_h, b_h, W1, b1, W2, b2, 
                 + [lambda: u0_c(t)]
             )
 
-        def warm(bank):
+        def mx_pass(c, i):
+            t = c * CH + (i % 16) // 4
+            m = i % 4
+            bank = pmm.tile([P, 512], F32, name="bank", tag="mm")
+            pp[(c, i)] = bank
+            if i < 16:
+                wc, ws, ac, asc = w1c, w1s, hq[t], hs[t]
+            else:
+                wc, ws, ac, asc = w2c, w2s, tq[t], ts[t]
             nc.tensor.matmul_mx(
-                out=bank,
-                lhsT=w1c[:, 0:P].bitcast(FP8X4),
-                lhsT_scale=w1s[:, 0:P],
-                rhs=w1c[:].bitcast(FP8X4),
-                rhs_scale=w1s[:],
+                out=bank[:],
+                lhsT=wc[:, m * P:(m + 1) * P].bitcast(FP8X4),
+                lhsT_scale=ws[:, m * P:(m + 1) * P],
+                rhs=ac[:].bitcast(FP8X4),
+                rhs_scale=asc[:],
                 start=True,
                 stop=True,
             )
 
-        def m1(t, m):
+        def act_er(c, i):
+            t = c * CH + i // 4
+            m = i % 4
             if m == 0:
                 ee[t] = work.tile([P, 4, 512], F32, name="ee", tag="ee", bufs=2)
                 rr[t] = work.tile([P, 4, 512], BF16, name="rr", tag="rr", bufs=2)
-            p1 = pmm.tile([P, 512], F32, name="p1", tag="mm")
-            warm(p1[:])
-            nc.tensor.matmul_mx(
-                out=p1[:],
-                lhsT=w1c[:, m * P:(m + 1) * P].bitcast(FP8X4),
-                lhsT_scale=w1s[:, m * P:(m + 1) * P],
-                rhs=hq[t][:].bitcast(FP8X4),
-                rhs_scale=hs[t][:],
-                start=True,
-                stop=True,
-            )
-            nc.scalar.activation(out=ee[t][:, m, :], in_=p1[:], func=ACTF.Exp, bias=b1e[:, m:m + 1], scale=1.0)
-            nc.scalar.activation(out=rr[t][:, m, :], in_=p1[:], func=ACTF.Relu, bias=sb1[:, m:m + 1], scale=SCALE)
+            bank = pp[(c, i)]
+            nc.scalar.activation(out=ee[t][:, m, :], in_=bank[:], func=ACTF.Exp, bias=b1e[:, m:m + 1], scale=1.0)
+            nc.scalar.activation(out=rr[t][:, m, :], in_=bank[:], func=ACTF.Relu, bias=sb1[:, m:m + 1], scale=SCALE)
+
+        def act_sig(c, i):
+            t = c * CH + i // 4
+            m = i % 4
+            if m == 0:
+                xx[t] = work.tile([P, 4, 512], F32, name="xx", tag="xx", bufs=4)
+            bank = pp[(c, 16 + i)]
+            nc.scalar.activation(out=xx[t][:, m, :], in_=bank[:], func=ACTF.Sigmoid, bias=nb2[:, m:m + 1], scale=-1.0)
 
         def c1(t):
             tpl = work.tile([P, 4, 512], BF16, name="tpl", tag="tpl", bufs=1)
@@ -226,65 +237,51 @@ def tile_decoder_t_kernel(tc, digits, styles, images, W_h, b_h, W1, b1, W2, b2, 
                 out=tq[t][:].bitcast(FP8X4), scales=ts[t][:], in_=tg[:].rearrange("p w j -> p (w j)")
             )
 
-        def m2(t, m):
-            if m == 0:
-                xx[t] = work.tile([P, 4, 512], F32, name="xx", tag="xx", bufs=4)
-            p2 = pmm.tile([P, 512], F32, name="p2", tag="mm")
-            nc.tensor.matmul_mx(
-                out=p2[:],
-                lhsT=w2c[:, m * P:(m + 1) * P].bitcast(FP8X4),
-                lhsT_scale=w2s[:, m * P:(m + 1) * P],
-                rhs=tq[t][:].bitcast(FP8X4),
-                rhs_scale=ts[t][:],
-                start=True,
-                stop=True,
-            )
-            nc.scalar.activation(out=xx[t][:, m, :], in_=p2[:], func=ACTF.Sigmoid, bias=bias[:, 8 + m:9 + m], scale=1.0)
-
         def ln(t):
-            aa[t] = work.tile([P, 4, 512], F32, name="aa", tag="aa", bufs=3)
-            bb[t] = work.tile([P, 4, 512], F32, name="bb", tag="bb", bufs=3)
+            aa[t] = work.tile([P, 4, 512], F32, name="aa", tag="aa", bufs=4)
+            bb[t] = work.tile([P, 4, 512], F32, name="bb", tag="bb", bufs=4)
             xf = xx[t][:].rearrange("p m w -> p (m w)")
             af = aa[t][:].rearrange("p m w -> p (m w)")
             bf = bb[t][:].rearrange("p m w -> p (m w)")
-            nc.scalar.activation(out=af, in_=xf, func=ACTF.Ln, bias=eps_t[:], scale=1.0)
-            nc.scalar.activation(out=bf, in_=xf, func=ACTF.Ln, bias=ope_t[:], scale=-1.0)
-            nc.gpsimd.tensor_tensor(out=bf, in0=bf, in1=af, op=ALU.subtract)
+            nc.scalar.activation(out=bf, in_=xf, func=ACTF.Ln, bias=eps_t[:], scale=1.0)
+            nc.scalar.activation(out=af, in_=xf, func=ACTF.Ln, bias=ope_t[:], scale=-1.0)
+            nc.gpsimd.tensor_tensor(out=af, in0=af, in1=bf, op=ALU.subtract)
 
         def im(t):
-            im1[t] = work.tile([P, 4, 512], F32, name="im1", tag="im1", bufs=4)
+            imp[t] = work.tile([P, 4, 512], BF16, name="imp", tag="imp", bufs=4)
             for s in range(4):
                 nc.gpsimd.tensor_scalar(
-                    out=im1[t][:, s, :].rearrange("p (m g r) -> p m g r", m=4, r=4),
+                    out=imp[t][:, s, :].rearrange("p (m g r) -> p m g r", m=4, r=4),
                     in0=img[t][:, s, :].rearrange("p (g m r) -> p m g r", m=4, r=4),
-                    scalar1=-1.0,
-                    scalar2=1.0,
+                    scalar1=1.0,
+                    scalar2=0.0,
                     op0=ALU.mult,
                     op1=ALU.add,
                 )
 
-        def tk(t, m):
-            imT = pim.tile([P, 4, P], F32, name="imT", tag="im")
-            warm(imT[:].rearrange("p s w -> p (s w)"))
-            for s in range(4):
-                nc.tensor.transpose(imT[:, s, :], im1[t][:, s, m * P:(m + 1) * P], idf[:])
+        def tk(t, h):
+            imT = psd.tile([P, 2, 4, P], BF16, name="imT", tag="sd")
+            for a in range(2):
+                for s in range(4):
+                    m = 2 * h + a
+                    nc.tensor.transpose(imT[:, a, s, :], imp[t][:, s, m * P:(m + 1) * P], idb[:])
+            kk = aa[t][:, 2 * h:2 * h + 2, :].rearrange("p a w -> p (a w)")
             nc.vector.scalar_tensor_tensor(
-                out=bb[t][:, m, :],
-                in0=bb[t][:, m, :],
+                out=kk,
+                in0=kk,
                 scalar=-DMAX,
-                in1=imT[:].rearrange("p s w -> p (s w)"),
+                in1=imT[:].rearrange("p a s w -> p (a s w)"),
                 op0=ALU.max,
                 op1=ALU.mult,
             )
 
         def ta(t, s):
             if s == 0:
-                acc[t] = pacc.tile([P, 4, P], F32, name="acc", tag="acc")
-                warm(acc[t][:].rearrange("p s w -> p (s w)"))
+                acc[t] = psd.tile([P, 4, P], F32, name="acc", tag="sd")
             for m in range(4):
                 nc.tensor.matmul(
                     out=acc[t][:, s, :],
-                    lhsT=aa[t][:, m, s * P:(s + 1) * P],
+                    lhsT=bb[t][:, m, s * P:(s + 1) * P],
                     rhs=idf[:],
                     is_transpose=True,
                     start=(m == 0),
@@ -293,7 +290,7 @@ def tile_decoder_t_kernel(tc, digits, styles, images, W_h, b_h, W1, b1, W2, b2, 
             for m in range(4):
                 nc.tensor.matmul(
                     out=acc[t][:, s, :],
-                    lhsT=bb[t][:, m, s * P:(s + 1) * P],
+                    lhsT=aa[t][:, m, s * P:(s + 1) * P],
                     rhs=idf[:],
                     is_transpose=True,
                     start=False,
@@ -312,12 +309,11 @@ def tile_decoder_t_kernel(tc, digits, styles, images, W_h, b_h, W1, b1, W2, b2, 
                 c = t // CH
                 nc.sync.dma_start(out=outv[:, 16 * c:16 * c + 16, :], in_=out_sb[:, 16 * c:16 * c + 16, :])
 
-        def tail(t):
-            for m in range(4):
-                tk(t, m)
-            for s in range(4):
-                ta(t, s)
-            tr(t)
+        def tk_pieces(t):
+            return [(lambda h: (lambda: tk(t, h)))(h) for h in range(2)]
+
+        def ta_pieces(t):
+            return [(lambda s: (lambda: ta(t, s)))(s) for s in range(4)] + [lambda: tr(t)]
 
         def run(pieces):
             for f in pieces:
@@ -325,50 +321,62 @@ def tile_decoder_t_kernel(tc, digits, styles, images, W_h, b_h, W1, b1, W2, b2, 
 
         run(u0_pieces(0))
         quant_w1()
+        for i in range(LA):
+            mx_pass(0, i)
         run(u0_pieces(1))
         quant_w2()
+        side = u0_pieces(2) + u0_pieces(3)
         for c in range(NCH):
             b = c * CH
             n = b + CH
             last = c == NCH - 1
             if not last:
                 ld_cat(c + 1)
-            for k in range(CH):
-                t = b + k
-                for m in range(4):
-                    m1(t, m)
-                    if c > 0 and k == 1:
-                        ta(b - 1, m)
-                if c == 0 and k < 2:
-                    run(u0_pieces(k + 2))
-                if c > 0 and k == 0:
-                    for m in range(4):
-                        tk(b - 1, m)
-                if c > 0 and k == 1:
-                    tr(b - 1)
-                c1(t)
-                im(t)
-                if t + 3 < NT:
-                    ld_img(t + 3)
-            fill = []
-            if not last:
-                fill = u0_pieces(n) + u0_pieces(n + 1)
+            per_step = 1
+            if c == 0:
+                per_step = 2
             used = 0
-            for i in range(4 * CH):
-                m2(b + i // 4, i % 4)
-                if i >= 3 and used < len(fill):
-                    fill[used]()
+            for i in range(16):
+                act_er(c, i)
+                mx_pass(c, i + LA)
+                for z in range(per_step):
+                    if used < len(side):
+                        side[used]()
+                        used += 1
+                if i % 4 == 3:
+                    t = b + i // 4
+                    c1(t)
+                    im(t)
+                    if t + 3 < NT:
+                        ld_img(t + 3)
+            run(side[used:])
+            side = []
+            if not last:
+                side = u0_pieces(n) + u0_pieces(n + 1)
+            used = 0
+            for i in range(16):
+                act_sig(c, i)
+                if 16 + i + LA < 32:
+                    mx_pass(c, 16 + i + LA)
+                if i >= 3 and used < len(side):
+                    side[used]()
                     used += 1
-            run(fill[used:])
+            run(side[used:])
+            if not last:
+                for i in range(LA):
+                    mx_pass(c + 1, i)
             ln(b)
             if not last:
                 run(u0_pieces(n + 2))
             ln(b + 1)
             if not last:
                 run(u0_pieces(n + 3))
-            tail(b)
+            run(tk_pieces(b))
             ln(b + 2)
-            tail(b + 1)
+            run(ta_pieces(b))
+            run(tk_pieces(b + 1))
             ln(b + 3)
-            tail(b + 2)
-        tail(NT - 1)
+            run(ta_pieces(b + 1))
+            run(tk_pieces(b + 2))
+            side = ta_pieces(b + 2) + tk_pieces(b + 3) + ta_pieces(b + 3)
+        run(side)

@@ -20,6 +20,8 @@ NB = 64
 NT = 16
 CH = 4
 NCH = 4
+IB = 6
+LN_EPS = math.log(1e-9)
 LA = 4
 FLOPS = 2 * 8192 * (128 * 512 + 2 * 512 * 512)
 
@@ -28,7 +30,6 @@ SCALE = 1.0507009873554804934193349852946
 SA = SCALE * ALPHA
 LN_SA = math.log(SA)
 EPS = 1e-9
-DMAX = math.log((1.0 + EPS) / EPS)
 
 
 def tile_decoder_t_kernel(tc, digits, styles, images, W_h, b_h, W1, b1, W2, b2, out):
@@ -58,7 +59,6 @@ def tile_decoder_t_kernel(tc, digits, styles, images, W_h, b_h, W1, b1, W2, b2, 
         aa = {}
         bb = {}
         img = {}
-        imp = {}
         pp = {}
         acc = {}
 
@@ -79,7 +79,7 @@ def tile_decoder_t_kernel(tc, digits, styles, images, W_h, b_h, W1, b1, W2, b2, 
             nc.sync.dma_start(out=cat[c][:, :, 32:128], in_=sty[:, 16 * c:16 * c + 16, :])
 
         def ld_img(t):
-            img[t] = work.tile([P, 4, 512], BF16, name="img", tag="img", bufs=3)
+            img[t] = work.tile([P, 4, 512], BF16, name="img", tag="img", bufs=IB)
             nc.sync.dma_start(out=img[t][:], in_=imgv[:, 4 * t:4 * t + 4, :])
 
         ld_cat(0)
@@ -87,27 +87,25 @@ def tile_decoder_t_kernel(tc, digits, styles, images, W_h, b_h, W1, b1, W2, b2, 
         nc.sync.dma_start(out=wh[:], in_=W_h)
         nc.sync.dma_start(out=brow[0:4, :], in_=b_h.rearrange("(j c) -> j c", j=4))
         nc.sync.dma_start(out=brow[4:8, :], in_=b1.rearrange("(j c) -> j c", j=4))
-        nc.sync.dma_start(
-            out=brow[8:12, :].rearrange("m (g r) -> m g r", r=4),
-            in_=b2.rearrange("(g m r) -> m g r", m=4, r=4),
-        )
+        b2raw = const.tile([P, 4], BF16, name="b2raw")
+        nc.sync.dma_start(out=b2raw[:], in_=b2.rearrange("(q m) -> q m", m=4))
         raw1 = work.tile([P, 4, 512], BF16, name="raw1", tag="raw", bufs=2)
         nc.sync.dma_start(out=raw1[:], in_=W1.rearrange("(j p) n -> p j n", p=P))
         raw2 = work.tile([P, 4, 512], BF16, name="raw2", tag="raw", bufs=2)
         nc.sync.dma_start(out=raw2[:], in_=W2.rearrange("(j p) n -> p j n", p=P))
-        for t in range(3):
+        for t in range(IB):
             ld_img(t)
 
         pb = psd.tile([P, P], BF16, name="pb", tag="sd")
         nc.tensor.transpose(pb[:], brow[:], idb[:])
-        bias = const.tile([P, 12], F32, name="bias")
-        nc.vector.tensor_copy(out=bias[:], in_=pb[:, 0:12])
+        bias = const.tile([P, 8], F32, name="bias")
+        nc.vector.tensor_copy(out=bias[:], in_=pb[:, 0:8])
         b1e = const.tile([P, 4], F32, name="b1e")
         sb1 = const.tile([P, 4], F32, name="sb1")
         nc.vector.tensor_scalar_add(out=b1e[:], in0=bias[:, 4:8], scalar1=LN_SA)
         nc.vector.tensor_scalar_mul(out=sb1[:], in0=bias[:, 4:8], scalar1=SCALE)
         nb2 = const.tile([P, 4], F32, name="nb2")
-        nc.vector.tensor_scalar_mul(out=nb2[:], in0=bias[:, 8:12], scalar1=-1.0)
+        nc.vector.tensor_scalar_mul(out=nb2[:], in0=b2raw[:], scalar1=-1.0)
         bh_bc = bias[:, 0:4].unsqueeze(1).to_broadcast([P, P, 4])
 
         w1c = const.tile([P, 512], U32, name="w1c", align_bytes=64)
@@ -122,12 +120,9 @@ def tile_decoder_t_kernel(tc, digits, styles, images, W_h, b_h, W1, b1, W2, b2, 
             in_=raw1[:].rearrange("p j (c i) -> p c j i", i=4),
         )
         grp2 = work.tile([P, 512, 4], BF16, name="grp2", tag="grp", bufs=2, align_bytes=64)
-        src2 = raw2[:].rearrange("p j (g m r) -> p m g j r", m=4, r=4)
+        src2 = raw2[:].rearrange("p j (q m) -> p m q j", m=4)
         for m in range(4):
-            nc.scalar.copy(
-                out=grp2[:, m * P:(m + 1) * P, :].rearrange("p (g r) j -> p g j r", r=4),
-                in_=src2[:, m],
-            )
+            nc.scalar.copy(out=grp2[:, m * P:(m + 1) * P, :], in_=src2[:, m])
 
         def quant_w1():
             nc.vector.quantize_mx(
@@ -245,35 +240,20 @@ def tile_decoder_t_kernel(tc, digits, styles, images, W_h, b_h, W1, b1, W2, b2, 
             bf = bb[t][:].rearrange("p m w -> p (m w)")
             nc.scalar.activation(out=bf, in_=xf, func=ACTF.Ln, bias=eps_t[:], scale=1.0)
             nc.scalar.activation(out=af, in_=xf, func=ACTF.Ln, bias=ope_t[:], scale=-1.0)
-            nc.gpsimd.tensor_tensor(out=af, in0=af, in1=bf, op=ALU.subtract)
 
-        def im(t):
-            imp[t] = work.tile([P, 4, 512], BF16, name="imp", tag="imp", bufs=4)
-            for s in range(4):
-                nc.gpsimd.tensor_scalar(
-                    out=imp[t][:, s, :].rearrange("p (m g r) -> p m g r", m=4, r=4),
-                    in0=img[t][:, s, :].rearrange("p (g m r) -> p m g r", m=4, r=4),
-                    scalar1=1.0,
-                    scalar2=0.0,
-                    op0=ALU.mult,
-                    op1=ALU.add,
-                )
+        def dd(t):
+            af = aa[t][:].rearrange("p m w -> p (m w)")
+            bf = bb[t][:].rearrange("p m w -> p (m w)")
+            nc.vector.scalar_tensor_tensor(out=af, in0=af, scalar=LN_EPS, in1=bf, op0=ALU.max, op1=ALU.subtract)
 
         def tk(t, h):
             imT = psd.tile([P, 2, 4, P], BF16, name="imT", tag="sd")
             for a in range(2):
                 for s in range(4):
                     m = 2 * h + a
-                    nc.tensor.transpose(imT[:, a, s, :], imp[t][:, s, m * P:(m + 1) * P], idb[:])
+                    nc.tensor.transpose(imT[:, a, s, :], img[t][:, s, :].rearrange("p (q m) -> p m q", m=4)[:, m, :], idb[:])
             kk = aa[t][:, 2 * h:2 * h + 2, :].rearrange("p a w -> p (a w)")
-            nc.vector.scalar_tensor_tensor(
-                out=kk,
-                in0=kk,
-                scalar=-DMAX,
-                in1=imT[:].rearrange("p a s w -> p (a s w)"),
-                op0=ALU.max,
-                op1=ALU.mult,
-            )
+            nc.vector.tensor_tensor(out=kk, in0=kk, in1=imT[:].rearrange("p a s w -> p (a s w)"), op=ALU.mult)
 
         def ta(t, s):
             if s == 0:
@@ -309,8 +289,12 @@ def tile_decoder_t_kernel(tc, digits, styles, images, W_h, b_h, W1, b1, W2, b2, 
                 c = t // CH
                 nc.sync.dma_start(out=outv[:, 16 * c:16 * c + 16, :], in_=out_sb[:, 16 * c:16 * c + 16, :])
 
+        def more_img(t):
+            if t + IB < NT:
+                ld_img(t + IB)
+
         def tk_pieces(t):
-            return [(lambda h: (lambda: tk(t, h)))(h) for h in range(2)]
+            return [lambda: dd(t)] + [(lambda h: (lambda: tk(t, h)))(h) for h in range(2)] + [lambda: more_img(t)]
 
         def ta_pieces(t):
             return [(lambda s: (lambda: ta(t, s)))(s) for s in range(4)] + [lambda: tr(t)]
@@ -346,9 +330,6 @@ def tile_decoder_t_kernel(tc, digits, styles, images, W_h, b_h, W1, b1, W2, b2, 
                 if i % 4 == 3:
                     t = b + i // 4
                     c1(t)
-                    im(t)
-                    if t + 3 < NT:
-                        ld_img(t + 3)
             run(side[used:])
             side = []
             if not last:

@@ -255,26 +255,20 @@ def tile_decoder_t_kernel(tc, digits, styles, images, W_h, b_h, W1, b1, W2, b2, 
             kk = aa[t][:, 2 * h:2 * h + 2, :].rearrange("p a w -> p (a w)")
             nc.vector.tensor_tensor(out=kk, in0=kk, in1=imT[:].rearrange("p a s w -> p (a s w)"), op=ALU.mult)
 
-        def ta(t, s):
-            if s == 0:
+        def ta(t, s, z):
+            if s == 0 and z == 0:
                 acc[t] = psd.tile([P, 4, P], F32, name="acc", tag="sd")
+            term = bb[t]
+            if z == 1:
+                term = aa[t]
             for m in range(4):
                 nc.tensor.matmul(
                     out=acc[t][:, s, :],
-                    lhsT=bb[t][:, m, s * P:(s + 1) * P],
+                    lhsT=term[:, m, s * P:(s + 1) * P],
                     rhs=idf[:],
                     is_transpose=True,
-                    start=(m == 0),
-                    stop=False,
-                )
-            for m in range(4):
-                nc.tensor.matmul(
-                    out=acc[t][:, s, :],
-                    lhsT=aa[t][:, m, s * P:(s + 1) * P],
-                    rhs=idf[:],
-                    is_transpose=True,
-                    start=False,
-                    stop=(m == 3),
+                    start=(z == 0 and m == 0),
+                    stop=(z == 1 and m == 3),
                 )
 
         def tr(t):
@@ -297,7 +291,7 @@ def tile_decoder_t_kernel(tc, digits, styles, images, W_h, b_h, W1, b1, W2, b2, 
             return [lambda: dd(t)] + [(lambda h: (lambda: tk(t, h)))(h) for h in range(2)] + [lambda: more_img(t)]
 
         def ta_pieces(t):
-            return [(lambda s: (lambda: ta(t, s)))(s) for s in range(4)] + [lambda: tr(t)]
+            return [(lambda i: (lambda: ta(t, i // 2, i % 2)))(i) for i in range(8)] + [lambda: tr(t)]
 
         def run(pieces):
             for f in pieces:
@@ -316,24 +310,19 @@ def tile_decoder_t_kernel(tc, digits, styles, images, W_h, b_h, W1, b1, W2, b2, 
             last = c == NCH - 1
             if not last:
                 ld_cat(c + 1)
-            per_step = 1
-            if c == 0:
-                per_step = 2
             used = 0
             for i in range(16):
                 act_er(c, i)
                 mx_pass(c, i + LA)
-                for z in range(per_step):
+                for z in range(2):
                     if used < len(side):
                         side[used]()
                         used += 1
                 if i % 4 == 3:
-                    t = b + i // 4
-                    c1(t)
-            run(side[used:])
-            side = []
+                    c1(b + i // 4)
+            side = side[used:]
             if not last:
-                side = u0_pieces(n) + u0_pieces(n + 1)
+                side = side + u0_pieces(n) + u0_pieces(n + 1)
             used = 0
             for i in range(16):
                 act_sig(c, i)
@@ -354,10 +343,17 @@ def tile_decoder_t_kernel(tc, digits, styles, images, W_h, b_h, W1, b1, W2, b2, 
                 run(u0_pieces(n + 3))
             run(tk_pieces(b))
             ln(b + 2)
-            run(ta_pieces(b))
             run(tk_pieces(b + 1))
+            if last:
+                run(ta_pieces(b))
             ln(b + 3)
-            run(ta_pieces(b + 1))
+            if not last:
+                run(ta_pieces(b))
             run(tk_pieces(b + 2))
-            side = ta_pieces(b + 2) + tk_pieces(b + 3) + ta_pieces(b + 3)
+            side = tk_pieces(b + 3)
+            if last:
+                run(ta_pieces(b + 1))
+            else:
+                side = side + ta_pieces(b + 1)
+            side = side + ta_pieces(b + 2) + ta_pieces(b + 3)
         run(side)

@@ -60,6 +60,7 @@ def tile_decoder_t_kernel(tc, digits, styles, images, W_h, b_h, W1, b1, W2, b2, 
         bb = {}
         img = {}
         pp = {}
+        tgs = {}
         acc = {}
 
         idb = const.tile([P, P], BF16, name="idb")
@@ -87,8 +88,8 @@ def tile_decoder_t_kernel(tc, digits, styles, images, W_h, b_h, W1, b1, W2, b2, 
         nc.sync.dma_start(out=wh[:], in_=W_h)
         nc.sync.dma_start(out=brow[0:4, :], in_=b_h.rearrange("(j c) -> j c", j=4))
         nc.sync.dma_start(out=brow[4:8, :], in_=b1.rearrange("(j c) -> j c", j=4))
-        b2raw = const.tile([P, 4], BF16, name="b2raw")
-        nc.sync.dma_start(out=b2raw[:], in_=b2.rearrange("(q m) -> q m", m=4))
+        b2raw = const.tile([P, 2, 2], BF16, name="b2raw")
+        nc.sync.dma_start(out=b2raw[:], in_=b2.rearrange("(h u e) -> u h e", h=2, e=2))
         raw1 = work.tile([P, 4, 512], BF16, name="raw1", tag="raw", bufs=2)
         nc.sync.dma_start(out=raw1[:], in_=W1.rearrange("(j p) n -> p j n", p=P))
         raw2 = work.tile([P, 4, 512], BF16, name="raw2", tag="raw", bufs=2)
@@ -105,7 +106,7 @@ def tile_decoder_t_kernel(tc, digits, styles, images, W_h, b_h, W1, b1, W2, b2, 
         nc.vector.tensor_scalar_add(out=b1e[:], in0=bias[:, 4:8], scalar1=LN_SA)
         nc.vector.tensor_scalar_mul(out=sb1[:], in0=bias[:, 4:8], scalar1=SCALE)
         nb2 = const.tile([P, 4], F32, name="nb2")
-        nc.vector.tensor_scalar_mul(out=nb2[:], in0=b2raw[:], scalar1=-1.0)
+        nc.vector.tensor_scalar_mul(out=nb2[:], in0=b2raw[:].rearrange("u h e -> u (h e)"), scalar1=-1.0)
         bh_bc = bias[:, 0:4].unsqueeze(1).to_broadcast([P, P, 4])
 
         w1c = const.tile([P, 512], U32, name="w1c", align_bytes=64)
@@ -120,9 +121,9 @@ def tile_decoder_t_kernel(tc, digits, styles, images, W_h, b_h, W1, b1, W2, b2, 
             in_=raw1[:].rearrange("p j (c i) -> p c j i", i=4),
         )
         grp2 = work.tile([P, 512, 4], BF16, name="grp2", tag="grp", bufs=2, align_bytes=64)
-        src2 = raw2[:].rearrange("p j (q m) -> p m q j", m=4)
+        src2 = raw2[:].rearrange("p j (h u e) -> p h e u j", h=2, e=2)
         for m in range(4):
-            nc.scalar.copy(out=grp2[:, m * P:(m + 1) * P, :], in_=src2[:, m])
+            nc.scalar.copy(out=grp2[:, m * P:(m + 1) * P, :], in_=src2[:, m // 2, m % 2])
 
         def quant_w1():
             nc.vector.quantize_mx(
@@ -163,16 +164,26 @@ def tile_decoder_t_kernel(tc, digits, styles, images, W_h, b_h, W1, b1, W2, b2, 
         def u0_c(t):
             flat = hg[t][:].rearrange("p w j -> p (w j)")
             nc.vector.tensor_scalar_max(out=flat, in0=flat, scalar1=0.0)
+
+        def u0_q(t):
+            flat = hg[t][:].rearrange("p w j -> p (w j)")
             hq[t] = work.tile([P, 512], U32, name="hq", tag="hq", bufs=4, align_bytes=64)
             hs[t] = work.tile([P, 512], U8, name="hs", tag="hs", bufs=4, align_bytes=64)
             nc.vector.quantize_mx(out=hq[t][:].bitcast(FP8X4), scales=hs[t][:], in_=flat)
 
-        def u0_pieces(t):
-            return (
-                [lambda: u0_a(t)]
-                + [(lambda s: (lambda: u0_b(t, s)))(s) for s in range(4)]
-                + [lambda: u0_c(t)]
-            )
+        def u0_stream(tiles):
+            pieces = [(lambda t: (lambda: u0_a(t)))(tiles[0])]
+            for i in range(len(tiles)):
+                t = tiles[i]
+                for s in range(4):
+                    if s == 2 and i + 1 < len(tiles):
+                        pieces.append((lambda t: (lambda: u0_a(t)))(tiles[i + 1]))
+                    pieces.append((lambda t, s: (lambda: u0_b(t, s)))(t, s))
+                    if s == 0 and i > 0:
+                        pieces.append((lambda t: (lambda: u0_q(t)))(tiles[i - 1]))
+                pieces.append((lambda t: (lambda: u0_c(t)))(t))
+            pieces.append((lambda t: (lambda: u0_q(t)))(tiles[len(tiles) - 1]))
+            return pieces
 
         def mx_pass(c, i):
             t = c * CH + (i % 16) // 4
@@ -226,6 +237,10 @@ def tile_decoder_t_kernel(tc, digits, styles, images, W_h, b_h, W1, b1, W2, b2, 
                 out=tg[:].rearrange("p (c i) j -> p c j i", i=4),
                 in_=tpl[:].rearrange("p j (c i) -> p c j i", i=4),
             )
+            tgs[t] = tg
+
+        def c1_q(t):
+            tg = tgs[t]
             tq[t] = work.tile([P, 512], U32, name="tq", tag="tq", bufs=4, align_bytes=64)
             ts[t] = work.tile([P, 512], U8, name="ts", tag="ts", bufs=4, align_bytes=64)
             nc.vector.quantize_mx(
@@ -247,41 +262,44 @@ def tile_decoder_t_kernel(tc, digits, styles, images, W_h, b_h, W1, b1, W2, b2, 
             nc.vector.scalar_tensor_tensor(out=af, in0=af, scalar=LN_EPS, in1=bf, op0=ALU.max, op1=ALU.subtract)
 
         def tk(t, h):
-            imT = psd.tile([P, 2, 4, P], BF16, name="imT", tag="sd")
-            for a in range(2):
-                for s in range(4):
-                    m = 2 * h + a
-                    nc.tensor.transpose(imT[:, a, s, :], img[t][:, s, :].rearrange("p (q m) -> p m q", m=4)[:, m, :], idb[:])
-            kk = aa[t][:, 2 * h:2 * h + 2, :].rearrange("p a w -> p (a w)")
-            nc.vector.tensor_tensor(out=kk, in0=kk, in1=imT[:].rearrange("p a s w -> p (a s w)"), op=ALU.mult)
+            imT = psd.tile([P, 4, P], F32, name="imT", tag="sd")
+            words = img[t][:].rearrange("p s x -> p (s x)").bitcast(F32)
+            for s in range(4):
+                nc.tensor.transpose(imT[:, s, :], words[:, s * 256 + h * P:s * 256 + (h + 1) * P], idf[:])
+            nc.vector.tensor_tensor(
+                out=aa[t][:, 2 * h:2 * h + 2, :],
+                in0=aa[t][:, 2 * h:2 * h + 2, :],
+                in1=imT[:].rearrange("p s w -> p (s w)").bitcast(BF16).rearrange("p (x e) -> p e x", e=2),
+                op=ALU.mult,
+            )
 
-        def ta(t, s, z):
-            if s == 0 and z == 0:
-                acc[t] = psd.tile([P, 4, P], F32, name="acc", tag="sd")
-            term = bb[t]
-            if z == 1:
-                term = aa[t]
-            for m in range(4):
+        def ta(t, s, h):
+            if s % 2 == 0 and h == 0:
+                acc[(t, s // 2)] = psd.tile([P, 2, 2, P], F32, name="acc", tag="sd")
+            terms = [bb[t][:, 2 * h, :], bb[t][:, 2 * h + 1, :], aa[t][:, 2 * h, :], aa[t][:, 2 * h + 1, :]]
+            for i in range(4):
                 nc.tensor.matmul(
-                    out=acc[t][:, s, :],
-                    lhsT=term[:, m, s * P:(s + 1) * P],
+                    out=acc[(t, s // 2)][:, s % 2, h, :],
+                    lhsT=terms[i][:, s * P:(s + 1) * P],
                     rhs=idf[:],
                     is_transpose=True,
-                    start=(z == 0 and m == 0),
-                    stop=(z == 1 and m == 3),
+                    start=(i == 0),
+                    stop=(i == 3),
                 )
 
-        def tr(t):
-            red = work.tile([P, P], F32, name="red", tag="red", bufs=2)
+        def tr(t, x):
             nc.vector.tensor_reduce(
-                out=red[:], in_=acc[t][:].rearrange("p s (g r) -> p (s g) r", r=4), axis=AX.X, op=ALU.add
+                out=out_sb[:, 4 * t + 2 * x:4 * t + 2 * x + 2, :].rearrange("p s g -> p (s g)"),
+                in_=acc[(t, x)][:].rearrange("p a h (g r) -> p (a h g) r", r=8),
+                axis=AX.X,
+                op=ALU.add,
             )
-            nc.vector.tensor_scalar_mul(
-                out=out_sb[:, 4 * t:4 * t + 4, :].rearrange("p s g -> p (s g)"), in0=red[:], scalar1=-1.0
-            )
-            if t % CH == CH - 1:
+            if t % CH == CH - 1 and x == 1:
                 c = t // CH
-                nc.sync.dma_start(out=outv[:, 16 * c:16 * c + 16, :], in_=out_sb[:, 16 * c:16 * c + 16, :])
+                chunk = out_sb[:, 16 * c:16 * c + 16, :]
+                flat = chunk.rearrange("p s g -> p (s g)")
+                nc.vector.tensor_scalar_mul(out=flat, in0=flat, scalar1=-1.0)
+                nc.sync.dma_start(out=outv[:, 16 * c:16 * c + 16, :], in_=chunk)
 
         def more_img(t):
             if t + IB < NT:
@@ -291,19 +309,26 @@ def tile_decoder_t_kernel(tc, digits, styles, images, W_h, b_h, W1, b1, W2, b2, 
             return [lambda: dd(t)] + [(lambda h: (lambda: tk(t, h)))(h) for h in range(2)] + [lambda: more_img(t)]
 
         def ta_pieces(t):
-            return [(lambda i: (lambda: ta(t, i // 2, i % 2)))(i) for i in range(8)] + [lambda: tr(t)]
+            pieces = []
+            for s in range(4):
+                pieces.append((lambda s: (lambda: ta(t, s, 0)))(s))
+                pieces.append((lambda s: (lambda: ta(t, s, 1)))(s))
+                if s % 2 == 1:
+                    pieces.append((lambda s: (lambda: tr(t, s // 2)))(s))
+            return pieces
 
         def run(pieces):
             for f in pieces:
                 f()
 
-        run(u0_pieces(0))
+        first = u0_stream([0, 1, 2, 3])
+        run(first[0:9])
         quant_w1()
         for i in range(LA):
             mx_pass(0, i)
-        run(u0_pieces(1))
+        run(first[9:16])
         quant_w2()
-        side = u0_pieces(2) + u0_pieces(3)
+        side = first[16:]
         for c in range(NCH):
             b = c * CH
             n = b + CH
@@ -318,11 +343,15 @@ def tile_decoder_t_kernel(tc, digits, styles, images, W_h, b_h, W1, b1, W2, b2, 
                     if used < len(side):
                         side[used]()
                         used += 1
+                if i % 4 == 0 and i > 0:
+                    c1_q(b + i // 4 - 1)
                 if i % 4 == 3:
                     c1(b + i // 4)
             side = side[used:]
+            nxt = []
             if not last:
-                side = side + u0_pieces(n) + u0_pieces(n + 1)
+                nxt = u0_stream([n, n + 1, n + 2, n + 3])
+            side = side + nxt[0:16]
             used = 0
             for i in range(16):
                 act_sig(c, i)
@@ -331,29 +360,25 @@ def tile_decoder_t_kernel(tc, digits, styles, images, W_h, b_h, W1, b1, W2, b2, 
                 if i >= 3 and used < len(side):
                     side[used]()
                     used += 1
+                if i == 4:
+                    c1_q(b + 3)
             run(side[used:])
             if not last:
                 for i in range(LA):
                     mx_pass(c + 1, i)
             ln(b)
-            if not last:
-                run(u0_pieces(n + 2))
+            run(nxt[16:22])
             ln(b + 1)
-            if not last:
-                run(u0_pieces(n + 3))
+            run(nxt[22:])
             run(tk_pieces(b))
             ln(b + 2)
             run(tk_pieces(b + 1))
-            if last:
-                run(ta_pieces(b))
             ln(b + 3)
-            if not last:
-                run(ta_pieces(b))
-            run(tk_pieces(b + 2))
-            side = tk_pieces(b + 3)
             if last:
-                run(ta_pieces(b + 1))
+                side = ta_pieces(b) + tk_pieces(b + 2) + ta_pieces(b + 1) + tk_pieces(b + 3)
             else:
-                side = side + ta_pieces(b + 1)
+                run(ta_pieces(b))
+                run(tk_pieces(b + 2))
+                side = tk_pieces(b + 3) + ta_pieces(b + 1)
             side = side + ta_pieces(b + 2) + ta_pieces(b + 3)
         run(side)

@@ -88,8 +88,8 @@ def tile_decoder_t_kernel(tc, digits, styles, images, W_h, b_h, W1, b1, W2, b2, 
         nc.sync.dma_start(out=wh[:], in_=W_h)
         nc.sync.dma_start(out=brow[0:4, :], in_=b_h.rearrange("(j c) -> j c", j=4))
         nc.sync.dma_start(out=brow[4:8, :], in_=b1.rearrange("(j c) -> j c", j=4))
-        b2raw = const.tile([P, 2, 2], BF16, name="b2raw")
-        nc.sync.dma_start(out=b2raw[:], in_=b2.rearrange("(h u e) -> u h e", h=2, e=2))
+        b2raw = const.tile([P, 4], BF16, name="b2raw")
+        nc.sync.dma_start(out=b2raw[:], in_=b2.rearrange("(q m) -> q m", m=4))
         raw1 = work.tile([P, 4, 512], BF16, name="raw1", tag="raw", bufs=2)
         nc.sync.dma_start(out=raw1[:], in_=W1.rearrange("(j p) n -> p j n", p=P))
         raw2 = work.tile([P, 4, 512], BF16, name="raw2", tag="raw", bufs=2)
@@ -106,7 +106,7 @@ def tile_decoder_t_kernel(tc, digits, styles, images, W_h, b_h, W1, b1, W2, b2, 
         nc.vector.tensor_scalar_add(out=b1e[:], in0=bias[:, 4:8], scalar1=LN_SA)
         nc.vector.tensor_scalar_mul(out=sb1[:], in0=bias[:, 4:8], scalar1=SCALE)
         nb2 = const.tile([P, 4], F32, name="nb2")
-        nc.vector.tensor_scalar_mul(out=nb2[:], in0=b2raw[:].rearrange("u h e -> u (h e)"), scalar1=-1.0)
+        nc.vector.tensor_scalar_mul(out=nb2[:], in0=b2raw[:], scalar1=-1.0)
         bh_bc = bias[:, 0:4].unsqueeze(1).to_broadcast([P, P, 4])
 
         w1c = const.tile([P, 512], U32, name="w1c", align_bytes=64)
@@ -121,9 +121,9 @@ def tile_decoder_t_kernel(tc, digits, styles, images, W_h, b_h, W1, b1, W2, b2, 
             in_=raw1[:].rearrange("p j (c i) -> p c j i", i=4),
         )
         grp2 = work.tile([P, 512, 4], BF16, name="grp2", tag="grp", bufs=2, align_bytes=64)
-        src2 = raw2[:].rearrange("p j (h u e) -> p h e u j", h=2, e=2)
+        src2 = raw2[:].rearrange("p j (q m) -> p m q j", m=4)
         for m in range(4):
-            nc.scalar.copy(out=grp2[:, m * P:(m + 1) * P, :], in_=src2[:, m // 2, m % 2])
+            nc.scalar.copy(out=grp2[:, m * P:(m + 1) * P, :], in_=src2[:, m])
 
         def quant_w1():
             nc.vector.quantize_mx(
@@ -265,7 +265,7 @@ def tile_decoder_t_kernel(tc, digits, styles, images, W_h, b_h, W1, b1, W2, b2, 
             imT = psd.tile([P, 4, P], F32, name="imT", tag="sd")
             words = img[t][:].rearrange("p s x -> p (s x)").bitcast(F32)
             for s in range(4):
-                nc.tensor.transpose(imT[:, s, :], words[:, s * 256 + h * P:s * 256 + (h + 1) * P], idf[:])
+                nc.tensor.transpose(imT[:, s, :], words[:, s * 256 + h:(s + 1) * 256:2], idf[:])
             nc.vector.tensor_tensor(
                 out=aa[t][:, 2 * h:2 * h + 2, :],
                 in0=aa[t][:, 2 * h:2 * h + 2, :],
@@ -273,28 +273,30 @@ def tile_decoder_t_kernel(tc, digits, styles, images, W_h, b_h, W1, b1, W2, b2, 
                 op=ALU.mult,
             )
 
-        def ta(t, s, h):
-            if s % 2 == 0 and h == 0:
-                acc[(t, s // 2)] = psd.tile([P, 2, 2, P], F32, name="acc", tag="sd")
-            terms = [bb[t][:, 2 * h, :], bb[t][:, 2 * h + 1, :], aa[t][:, 2 * h, :], aa[t][:, 2 * h + 1, :]]
-            for i in range(4):
+        def ta(t, s, z):
+            if s == 0 and z == 0:
+                acc[t] = psd.tile([P, 4, P], F32, name="acc", tag="sd")
+            term = bb[t]
+            if z == 1:
+                term = aa[t]
+            for m in range(4):
                 nc.tensor.matmul(
-                    out=acc[(t, s // 2)][:, s % 2, h, :],
-                    lhsT=terms[i][:, s * P:(s + 1) * P],
+                    out=acc[t][:, s, :],
+                    lhsT=term[:, m, s * P:(s + 1) * P],
                     rhs=idf[:],
                     is_transpose=True,
-                    start=(i == 0),
-                    stop=(i == 3),
+                    start=(z == 0 and m == 0),
+                    stop=(z == 1 and m == 3),
                 )
 
-        def tr(t, x):
+        def tr(t):
             nc.vector.tensor_reduce(
-                out=out_sb[:, 4 * t + 2 * x:4 * t + 2 * x + 2, :].rearrange("p s g -> p (s g)"),
-                in_=acc[(t, x)][:].rearrange("p a h (g r) -> p (a h g) r", r=8),
+                out=out_sb[:, 4 * t:4 * t + 4, :].rearrange("p s g -> p (s g)"),
+                in_=acc[t][:].rearrange("p s (g r) -> p (s g) r", r=4),
                 axis=AX.X,
                 op=ALU.add,
             )
-            if t % CH == CH - 1 and x == 1:
+            if t % CH == CH - 1:
                 c = t // CH
                 chunk = out_sb[:, 16 * c:16 * c + 16, :]
                 flat = chunk.rearrange("p s g -> p (s g)")
@@ -313,8 +315,7 @@ def tile_decoder_t_kernel(tc, digits, styles, images, W_h, b_h, W1, b1, W2, b2, 
             for s in range(4):
                 pieces.append((lambda s: (lambda: ta(t, s, 0)))(s))
                 pieces.append((lambda s: (lambda: ta(t, s, 1)))(s))
-                if s % 2 == 1:
-                    pieces.append((lambda s: (lambda: tr(t, s // 2)))(s))
+            pieces.append(lambda: tr(t))
             return pieces
 
         def run(pieces):

@@ -40,7 +40,6 @@ def tile_decoder_t_kernel(tc, digits, styles, images, W_h, b_h, W1, b1, W2, b2, 
     outv = out.rearrange("s b c h -> (s b) (c h)").rearrange("(p n) g -> p n g", n=NB)
 
     with ExitStack() as ctx:
-        ctx.enter_context(tc.manual_schedule())
         const = ctx.enter_context(tc.tile_pool(name="const", bufs=1))
         work = ctx.enter_context(tc.tile_pool(name="work", bufs=2))
         pmm = ctx.enter_context(tc.psum_pool(name="pmm", bufs=LA))
@@ -88,8 +87,8 @@ def tile_decoder_t_kernel(tc, digits, styles, images, W_h, b_h, W1, b1, W2, b2, 
         nc.sync.dma_start(out=wh[:], in_=W_h)
         nc.sync.dma_start(out=brow[0:4, :], in_=b_h.rearrange("(j c) -> j c", j=4))
         nc.sync.dma_start(out=brow[4:8, :], in_=b1.rearrange("(j c) -> j c", j=4))
-        b2raw = const.tile([P, 4], BF16, name="b2raw")
-        nc.sync.dma_start(out=b2raw[:], in_=b2.rearrange("(q m) -> q m", m=4))
+        b2raw = const.tile([P, 2, 2], BF16, name="b2raw")
+        nc.sync.dma_start(out=b2raw[:], in_=b2.rearrange("(h u e) -> u h e", h=2, e=2))
         raw1 = work.tile([P, 4, 512], BF16, name="raw1", tag="raw", bufs=2)
         nc.sync.dma_start(out=raw1[:], in_=W1.rearrange("(j p) n -> p j n", p=P))
         raw2 = work.tile([P, 4, 512], BF16, name="raw2", tag="raw", bufs=2)
@@ -106,7 +105,7 @@ def tile_decoder_t_kernel(tc, digits, styles, images, W_h, b_h, W1, b1, W2, b2, 
         nc.vector.tensor_scalar_add(out=b1e[:], in0=bias[:, 4:8], scalar1=LN_SA)
         nc.vector.tensor_scalar_mul(out=sb1[:], in0=bias[:, 4:8], scalar1=SCALE)
         nb2 = const.tile([P, 4], F32, name="nb2")
-        nc.vector.tensor_scalar_mul(out=nb2[:], in0=b2raw[:], scalar1=-1.0)
+        nc.vector.tensor_scalar_mul(out=nb2[:], in0=b2raw[:].rearrange("u h e -> u (h e)"), scalar1=-1.0)
         bh_bc = bias[:, 0:4].unsqueeze(1).to_broadcast([P, P, 4])
 
         w1c = const.tile([P, 512], U32, name="w1c", align_bytes=64)
@@ -121,9 +120,9 @@ def tile_decoder_t_kernel(tc, digits, styles, images, W_h, b_h, W1, b1, W2, b2, 
             in_=raw1[:].rearrange("p j (c i) -> p c j i", i=4),
         )
         grp2 = work.tile([P, 512, 4], BF16, name="grp2", tag="grp", bufs=2, align_bytes=64)
-        src2 = raw2[:].rearrange("p j (q m) -> p m q j", m=4)
+        src2 = raw2[:].rearrange("p j (h u e) -> p h e u j", h=2, e=2)
         for m in range(4):
-            nc.scalar.copy(out=grp2[:, m * P:(m + 1) * P, :], in_=src2[:, m])
+            nc.scalar.copy(out=grp2[:, m * P:(m + 1) * P, :], in_=src2[:, m // 2, m % 2])
 
         def quant_w1():
             nc.vector.quantize_mx(
@@ -265,7 +264,7 @@ def tile_decoder_t_kernel(tc, digits, styles, images, W_h, b_h, W1, b1, W2, b2, 
             imT = psd.tile([P, 4, P], F32, name="imT", tag="sd")
             words = img[t][:].rearrange("p s x -> p (s x)").bitcast(F32)
             for s in range(4):
-                nc.tensor.transpose(imT[:, s, :], words[:, s * 256 + h:(s + 1) * 256:2], idf[:])
+                nc.tensor.transpose(imT[:, s, :], words[:, s * 256 + h * P:s * 256 + (h + 1) * P], idf[:])
             nc.vector.tensor_tensor(
                 out=aa[t][:, 2 * h:2 * h + 2, :],
                 in0=aa[t][:, 2 * h:2 * h + 2, :],
@@ -273,30 +272,28 @@ def tile_decoder_t_kernel(tc, digits, styles, images, W_h, b_h, W1, b1, W2, b2, 
                 op=ALU.mult,
             )
 
-        def ta(t, s, z):
-            if s == 0 and z == 0:
-                acc[t] = psd.tile([P, 4, P], F32, name="acc", tag="sd")
-            term = bb[t]
-            if z == 1:
-                term = aa[t]
-            for m in range(4):
+        def ta(t, s, h):
+            if s % 2 == 0 and h == 0:
+                acc[(t, s // 2)] = psd.tile([P, 2, 2, P], F32, name="acc", tag="sd")
+            terms = [bb[t][:, 2 * h, :], bb[t][:, 2 * h + 1, :], aa[t][:, 2 * h, :], aa[t][:, 2 * h + 1, :]]
+            for i in range(4):
                 nc.tensor.matmul(
-                    out=acc[t][:, s, :],
-                    lhsT=term[:, m, s * P:(s + 1) * P],
+                    out=acc[(t, s // 2)][:, s % 2, h, :],
+                    lhsT=terms[i][:, s * P:(s + 1) * P],
                     rhs=idf[:],
                     is_transpose=True,
-                    start=(z == 0 and m == 0),
-                    stop=(z == 1 and m == 3),
+                    start=(i == 0),
+                    stop=(i == 3),
                 )
 
-        def tr(t):
+        def tr(t, x):
             nc.vector.tensor_reduce(
-                out=out_sb[:, 4 * t:4 * t + 4, :].rearrange("p s g -> p (s g)"),
-                in_=acc[t][:].rearrange("p s (g r) -> p (s g) r", r=4),
+                out=out_sb[:, 4 * t + 2 * x:4 * t + 2 * x + 2, :].rearrange("p s g -> p (s g)"),
+                in_=acc[(t, x)][:].rearrange("p a h (g r) -> p (a h g) r", r=8),
                 axis=AX.X,
                 op=ALU.add,
             )
-            if t % CH == CH - 1:
+            if t % CH == CH - 1 and x == 1:
                 c = t // CH
                 chunk = out_sb[:, 16 * c:16 * c + 16, :]
                 flat = chunk.rearrange("p s g -> p (s g)")
@@ -315,7 +312,8 @@ def tile_decoder_t_kernel(tc, digits, styles, images, W_h, b_h, W1, b1, W2, b2, 
             for s in range(4):
                 pieces.append((lambda s: (lambda: ta(t, s, 0)))(s))
                 pieces.append((lambda s: (lambda: ta(t, s, 1)))(s))
-            pieces.append(lambda: tr(t))
+                if s % 2 == 1:
+                    pieces.append((lambda s: (lambda: tr(t, s // 2)))(s))
             return pieces
 
         def run(pieces):

@@ -222,19 +222,14 @@ def tile_decoder_t_kernel(tc, digits, styles, images, W_h, b_h, W1, b1, W2, b2, 
             nc.scalar.activation(out=xx[t][:, m, :], in_=bank[:], func=ACTF.Sigmoid, bias=nb2[:, m:m + 1], scale=-1.0)
 
         def c1(t):
-            tpl = work.tile([P, 4, 512], BF16, name="tpl", tag="tpl", bufs=1)
+            tg = work.tile([P, 512, 4], BF16, name="tg", tag="tg", bufs=2, align_bytes=64)
             nc.vector.scalar_tensor_tensor(
-                out=tpl[:].rearrange("p m w -> p (m w)"),
-                in0=ee[t][:].rearrange("p m w -> p (m w)"),
+                out=tg[:],
+                in0=ee[t][:].rearrange("p j w -> p w j"),
                 scalar=SA,
-                in1=rr[t][:].rearrange("p m w -> p (m w)"),
+                in1=rr[t][:].rearrange("p j w -> p w j"),
                 op0=ALU.subtract,
                 op1=ALU.min,
-            )
-            tg = work.tile([P, 512, 4], BF16, name="tg", tag="tg", bufs=2, align_bytes=64)
-            nc.vector.tensor_copy(
-                out=tg[:].rearrange("p (c i) j -> p c j i", i=4),
-                in_=tpl[:].rearrange("p j (c i) -> p c j i", i=4),
             )
             tgs[t] = tg
 

@@ -87,8 +87,8 @@ def tile_decoder_t_kernel(tc, digits, styles, images, W_h, b_h, W1, b1, W2, b2, 
         nc.sync.dma_start(out=wh[:], in_=W_h)
         nc.sync.dma_start(out=brow[0:4, :], in_=b_h.rearrange("(j c) -> j c", j=4))
         nc.sync.dma_start(out=brow[4:8, :], in_=b1.rearrange("(j c) -> j c", j=4))
-        b2raw = const.tile([P, 2, 2], BF16, name="b2raw")
-        nc.sync.dma_start(out=b2raw[:], in_=b2.rearrange("(h u e) -> u h e", h=2, e=2))
+        b2raw = const.tile([P, 4], BF16, name="b2raw")
+        nc.sync.dma_start(out=b2raw[:], in_=b2.rearrange("(q m) -> q m", m=4))
         raw1 = work.tile([P, 4, 512], BF16, name="raw1", tag="raw", bufs=2)
         nc.sync.dma_start(out=raw1[:], in_=W1.rearrange("(j p) n -> p j n", p=P))
         raw2 = work.tile([P, 4, 512], BF16, name="raw2", tag="raw", bufs=2)
@@ -105,7 +105,7 @@ def tile_decoder_t_kernel(tc, digits, styles, images, W_h, b_h, W1, b1, W2, b2, 
         nc.vector.tensor_scalar_add(out=b1e[:], in0=bias[:, 4:8], scalar1=LN_SA)
         nc.vector.tensor_scalar_mul(out=sb1[:], in0=bias[:, 4:8], scalar1=SCALE)
         nb2 = const.tile([P, 4], F32, name="nb2")
-        nc.vector.tensor_scalar_mul(out=nb2[:], in0=b2raw[:].rearrange("u h e -> u (h e)"), scalar1=-1.0)
+        nc.vector.tensor_scalar_mul(out=nb2[:], in0=b2raw[:], scalar1=-1.0)
         bh_bc = bias[:, 0:4].unsqueeze(1).to_broadcast([P, P, 4])
 
         w1c = const.tile([P, 512], U32, name="w1c", align_bytes=64)
@@ -120,9 +120,9 @@ def tile_decoder_t_kernel(tc, digits, styles, images, W_h, b_h, W1, b1, W2, b2, 
             in_=raw1[:].rearrange("p j (c i) -> p c j i", i=4),
         )
         grp2 = work.tile([P, 512, 4], BF16, name="grp2", tag="grp", bufs=2, align_bytes=64)
-        src2 = raw2[:].rearrange("p j (h u e) -> p h e u j", h=2, e=2)
+        src2 = raw2[:].rearrange("p j (q m) -> p m q j", m=4)
         for m in range(4):
-            nc.scalar.copy(out=grp2[:, m * P:(m + 1) * P, :], in_=src2[:, m // 2, m % 2])
+            nc.scalar.copy(out=grp2[:, m * P:(m + 1) * P, :], in_=src2[:, m])
 
         def quant_w1():
             nc.vector.quantize_mx(
@@ -259,7 +259,7 @@ def tile_decoder_t_kernel(tc, digits, styles, images, W_h, b_h, W1, b1, W2, b2, 
             imT = psd.tile([P, 4, P], F32, name="imT", tag="sd")
             words = img[t][:].rearrange("p s x -> p (s x)").bitcast(F32)
             for s in range(4):
-                nc.tensor.transpose(imT[:, s, :], words[:, s * 256 + h * P:s * 256 + (h + 1) * P], idf[:])
+                nc.tensor.transpose(imT[:, s, :], words[:, s * 256 + h:(s + 1) * 256:2], idf[:])
             nc.vector.tensor_tensor(
                 out=aa[t][:, 2 * h:2 * h + 2, :],
                 in0=aa[t][:, 2 * h:2 * h + 2, :],
@@ -267,28 +267,28 @@ def tile_decoder_t_kernel(tc, digits, styles, images, W_h, b_h, W1, b1, W2, b2, 
                 op=ALU.mult,
             )
 
-        def ta(t, s, h):
-            if s % 2 == 0 and h == 0:
-                acc[(t, s // 2)] = psd.tile([P, 2, 2, P], F32, name="acc", tag="sd")
-            terms = [bb[t][:, 2 * h, :], bb[t][:, 2 * h + 1, :], aa[t][:, 2 * h, :], aa[t][:, 2 * h + 1, :]]
-            for i in range(4):
+        def ta(t, s):
+            if s == 0:
+                acc[t] = psd.tile([P, 4, P], F32, name="acc", tag="sd")
+            terms = [bb[t][:, m, :] for m in range(4)] + [aa[t][:, m, :] for m in range(4)]
+            for i in range(8):
                 nc.tensor.matmul(
-                    out=acc[(t, s // 2)][:, s % 2, h, :],
+                    out=acc[t][:, s, :],
                     lhsT=terms[i][:, s * P:(s + 1) * P],
                     rhs=idf[:],
                     is_transpose=True,
                     start=(i == 0),
-                    stop=(i == 3),
+                    stop=(i == 7),
                 )
 
-        def tr(t, x):
+        def tr(t):
             nc.vector.tensor_reduce(
-                out=out_sb[:, 4 * t + 2 * x:4 * t + 2 * x + 2, :].rearrange("p s g -> p (s g)"),
-                in_=acc[(t, x)][:].rearrange("p a h (g r) -> p (a h g) r", r=8),
+                out=out_sb[:, 4 * t:4 * t + 4, :].rearrange("p s g -> p (s g)"),
+                in_=acc[t][:].rearrange("p s (g r) -> p (s g) r", r=4),
                 axis=AX.X,
                 op=ALU.add,
             )
-            if t % CH == CH - 1 and x == 1:
+            if t % CH == CH - 1:
                 c = t // CH
                 chunk = out_sb[:, 16 * c:16 * c + 16, :]
                 flat = chunk.rearrange("p s g -> p (s g)")
@@ -305,10 +305,8 @@ def tile_decoder_t_kernel(tc, digits, styles, images, W_h, b_h, W1, b1, W2, b2, 
         def ta_pieces(t):
             pieces = []
             for s in range(4):
-                pieces.append((lambda s: (lambda: ta(t, s, 0)))(s))
-                pieces.append((lambda s: (lambda: ta(t, s, 1)))(s))
-                if s % 2 == 1:
-                    pieces.append((lambda s: (lambda: tr(t, s // 2)))(s))
+                pieces.append((lambda s: (lambda: ta(t, s)))(s))
+            pieces.append(lambda: tr(t))
             return pieces
 
         def run(pieces):

@@ -68,29 +68,42 @@ def tile_decoder_t_kernel(tc, digits, styles, images, W_h, b_h, W1, b1, W2, b2, 
         make_identity(nc, idf[:])
         brow = const.tile([P, P], BF16, name="brow")
         nc.vector.memset(brow[:], 0.0)
+        brow2 = const.tile([P, P], BF16, name="brow2")
+        nc.vector.memset(brow2[:], 0.0)
+        sel = const.tile([P, 4, P], BF16, name="sel")
+        nc.vector.tensor_copy(out=sel[:], in_=idb[:, 0:4].unsqueeze(2).to_broadcast([P, 4, P]))
         eps_t = const.tile([P, 1], F32, name="eps_t")
         ope_t = const.tile([P, 1], F32, name="ope_t")
         nc.vector.memset(eps_t[:], EPS)
         nc.vector.tensor_scalar_add(out=ope_t[:], in0=eps_t[:], scalar1=1.0)
 
+        exp_t = const.tile([P, 1], F32, name="exp_t")
+        nc.scalar.activation(out=exp_t[:], in_=eps_t[:], func=ACTF.Exp)
+
         def ld_cat(c):
             cat[c] = work.tile([P, 16, P], BF16, name="cat", tag="cat", bufs=2)
-            nc.sync.dma_start(out=cat[c][:, :, 0:32], in_=dig[:, 16 * c:16 * c + 16, :])
-            nc.sync.dma_start(out=cat[c][:, :, 32:128], in_=sty[:, 16 * c:16 * c + 16, :])
+            ld_cat_blocks(c, 0, 16)
+
+        def ld_cat_blocks(c, x, y):
+            nc.sync.dma_start(out=cat[c][:, x:y, 0:32], in_=dig[:, 16 * c + x:16 * c + y, :])
+            nc.sync.dma_start(out=cat[c][:, x:y, 32:128], in_=sty[:, 16 * c + x:16 * c + y, :])
 
         def ld_img(t):
             img[t] = work.tile([P, 4, 512], BF16, name="img", tag="img", bufs=IB)
             nc.sync.dma_start(out=img[t][:], in_=imgv[:, 4 * t:4 * t + 4, :])
 
-        ld_cat(0)
+        cat[0] = work.tile([P, 16, P], BF16, name="cat", tag="cat", bufs=2)
+        ld_cat_blocks(0, 0, 4)
         wh = const.tile([P, 512], BF16, name="wh")
         nc.sync.dma_start(out=wh[:], in_=W_h)
         nc.sync.dma_start(out=brow[0:4, :], in_=b_h.rearrange("(j c) -> j c", j=4))
         nc.sync.dma_start(out=brow[4:8, :], in_=b1.rearrange("(j c) -> j c", j=4))
+        nc.sync.dma_start(out=brow2[0:4, :], in_=b_h.rearrange("(j c) -> j c", j=4))
         b2raw = const.tile([P, 4], BF16, name="b2raw")
         nc.sync.dma_start(out=b2raw[:], in_=b2.rearrange("(q m) -> q m", m=4))
         raw1 = work.tile([P, 4, 512], BF16, name="raw1", tag="raw", bufs=2)
         nc.sync.dma_start(out=raw1[:], in_=W1.rearrange("(j p) n -> p j n", p=P))
+        ld_cat_blocks(0, 4, 16)
         raw2 = work.tile([P, 4, 512], BF16, name="raw2", tag="raw", bufs=2)
         nc.sync.dma_start(out=raw2[:], in_=W2.rearrange("(j p) n -> p j n", p=P))
         for t in range(IB):
@@ -145,14 +158,28 @@ def tile_decoder_t_kernel(tc, digits, styles, images, W_h, b_h, W1, b1, W2, b2, 
 
         def u0_b(t, s):
             p0 = psd.tile([P, 4, P], F32, name="p0", tag="sd")
+            biased = t in range(8)
+            if biased:
+                nc.tensor.matmul(
+                    out=p0[:].rearrange("p j w -> p (j w)"),
+                    lhsT=brow2[:],
+                    rhs=sel[:].rearrange("p j w -> p (j w)"),
+                    start=True,
+                    stop=False,
+                )
             for j in range(4):
                 nc.tensor.matmul(
                     out=p0[:, j, :],
                     lhsT=wh[:, j * P:(j + 1) * P],
                     rhs=catT[t][:, s * P:(s + 1) * P],
-                    start=True,
-                    stop=True,
+                    start=not biased,
+                    stop=not biased or j == 3,
                 )
+            if biased:
+                nc.vector.tensor_scalar_max(
+                    out=hg[t][:, s * P:(s + 1) * P, :], in0=p0[:].rearrange("p j w -> p w j"), scalar1=0.0
+                )
+                return
             nc.vector.tensor_tensor(
                 out=hg[t][:, s * P:(s + 1) * P, :],
                 in0=p0[:].rearrange("p j w -> p w j"),
@@ -161,6 +188,8 @@ def tile_decoder_t_kernel(tc, digits, styles, images, W_h, b_h, W1, b1, W2, b2, 
             )
 
         def u0_c(t):
+            if t in range(8):
+                return
             flat = hg[t][:].rearrange("p w j -> p (w j)")
             nc.vector.tensor_scalar_max(out=flat, in0=flat, scalar1=0.0)
 
@@ -287,12 +316,11 @@ def tile_decoder_t_kernel(tc, digits, styles, images, W_h, b_h, W1, b1, W2, b2, 
                 in_=acc[t][:].rearrange("p s (g r) -> p (s g) r", r=4),
                 axis=AX.X,
                 op=ALU.add,
+                negate=True,
             )
             if t % CH == CH - 1:
                 c = t // CH
                 chunk = out_sb[:, 16 * c:16 * c + 16, :]
-                flat = chunk.rearrange("p s g -> p (s g)")
-                nc.vector.tensor_scalar_mul(out=flat, in0=flat, scalar1=-1.0)
                 nc.sync.dma_start(out=outv[:, 16 * c:16 * c + 16, :], in_=chunk)
 
         def more_img(t):
@@ -313,14 +341,17 @@ def tile_decoder_t_kernel(tc, digits, styles, images, W_h, b_h, W1, b1, W2, b2, 
             for f in pieces:
                 f()
 
-        first = u0_stream([0, 1, 2, 3])
-        run(first[0:9])
+        run(u0_stream([0])[0:5])
+        u0_a(1)
         quant_w1()
+        u0_c(0)
+        u0_q(0)
         for i in range(LA):
             mx_pass(0, i)
-        run(first[9:16])
+        first = u0_stream([1, 2, 3])[1:]
+        run(first[0:8])
         quant_w2()
-        side = first[16:]
+        side = first[8:]
         for c in range(NCH):
             b = c * CH
             n = b + CH

@@ -18,9 +18,8 @@ AX = mybir.AxisListType
 P = 128
 NB = 64
 NT = 16
-CH = 4
-NCH = 4
-IB = 6
+CHUNKS = [4, 6, 6]
+IB = 5
 LN_EPS = math.log(1e-9)
 LA = 4
 FLOPS = 2 * 8192 * (128 * 512 + 2 * 512 * 512)
@@ -40,6 +39,7 @@ def tile_decoder_t_kernel(tc, digits, styles, images, W_h, b_h, W1, b1, W2, b2, 
     outv = out.rearrange("s b c h -> (s b) (c h)").rearrange("(p n) g -> p n g", n=NB)
 
     with ExitStack() as ctx:
+        ctx.enter_context(tc.manual_schedule(engines={mybir.EngineType.Activation}))
         const = ctx.enter_context(tc.tile_pool(name="const", bufs=1))
         work = ctx.enter_context(tc.tile_pool(name="work", bufs=2))
         pmm = ctx.enter_context(tc.psum_pool(name="pmm", bufs=LA))
@@ -81,19 +81,25 @@ def tile_decoder_t_kernel(tc, digits, styles, images, W_h, b_h, W1, b1, W2, b2, 
         nc.scalar.activation(out=exp_t[:], in_=eps_t[:], func=ACTF.Exp)
 
         def ld_cat(c):
-            cat[c] = work.tile([P, 16, P], BF16, name="cat", tag="cat", bufs=2)
-            ld_cat_blocks(c, 0, 16)
+            n = 4 * CHUNKS[c]
+            x = 4 * sum(CHUNKS[:c])
+            blocks = work.tile([P, n, P], BF16, name="cat", tag="cat", bufs=2)
+            for t in range(CHUNKS[c]):
+                cat[x // 4 + t] = blocks[:, 4 * t:4 * t + 4, :]
+            if c > 0:
+                ld_cat_blocks(blocks, x, 0, n)
+            return blocks
 
-        def ld_cat_blocks(c, x, y):
-            nc.sync.dma_start(out=cat[c][:, x:y, 0:32], in_=dig[:, 16 * c + x:16 * c + y, :])
-            nc.sync.dma_start(out=cat[c][:, x:y, 32:128], in_=sty[:, 16 * c + x:16 * c + y, :])
+        def ld_cat_blocks(blocks, x, u, v):
+            nc.sync.dma_start(out=blocks[:, u:v, 0:32], in_=dig[:, x + u:x + v, :])
+            nc.sync.dma_start(out=blocks[:, u:v, 32:128], in_=sty[:, x + u:x + v, :])
 
         def ld_img(t):
             img[t] = work.tile([P, 4, 512], BF16, name="img", tag="img", bufs=IB)
             nc.sync.dma_start(out=img[t][:], in_=imgv[:, 4 * t:4 * t + 4, :])
 
-        cat[0] = work.tile([P, 16, P], BF16, name="cat", tag="cat", bufs=2)
-        ld_cat_blocks(0, 0, 4)
+        first_blocks = ld_cat(0)
+        ld_cat_blocks(first_blocks, 0, 0, 4)
         wh = const.tile([P, 512], BF16, name="wh")
         nc.sync.dma_start(out=wh[:], in_=W_h)
         nc.sync.dma_start(out=brow[0:4, :], in_=b_h.rearrange("(j c) -> j c", j=4))
@@ -103,23 +109,26 @@ def tile_decoder_t_kernel(tc, digits, styles, images, W_h, b_h, W1, b1, W2, b2, 
         nc.sync.dma_start(out=b2raw[:], in_=b2.rearrange("(q m) -> q m", m=4))
         raw1 = work.tile([P, 4, 512], BF16, name="raw1", tag="raw", bufs=2)
         nc.sync.dma_start(out=raw1[:], in_=W1.rearrange("(j p) n -> p j n", p=P))
-        ld_cat_blocks(0, 4, 16)
+        ld_cat_blocks(first_blocks, 0, 4, 4 * CHUNKS[0])
         raw2 = work.tile([P, 4, 512], BF16, name="raw2", tag="raw", bufs=2)
         nc.sync.dma_start(out=raw2[:], in_=W2.rearrange("(j p) n -> p j n", p=P))
         for t in range(IB):
             ld_img(t)
 
-        pb = psd.tile([P, P], BF16, name="pb", tag="sd")
-        nc.tensor.transpose(pb[:], brow[:], idb[:])
         bias = const.tile([P, 8], F32, name="bias")
-        nc.vector.tensor_copy(out=bias[:], in_=pb[:, 0:8])
         b1e = const.tile([P, 4], F32, name="b1e")
         sb1 = const.tile([P, 4], F32, name="sb1")
-        nc.vector.tensor_scalar_add(out=b1e[:], in0=bias[:, 4:8], scalar1=LN_SA)
-        nc.vector.tensor_scalar_mul(out=sb1[:], in0=bias[:, 4:8], scalar1=SCALE)
+        bh_bc = bias[:, 0:4].unsqueeze(1).to_broadcast([P, P, 4])
+
+        def biases():
+            pb = psd.tile([P, P], BF16, name="pb", tag="sd")
+            nc.tensor.transpose(pb[:], brow[:], idb[:])
+            nc.vector.tensor_copy(out=bias[:], in_=pb[:, 0:8])
+            nc.vector.tensor_scalar_add(out=b1e[:], in0=bias[:, 4:8], scalar1=LN_SA)
+            nc.vector.tensor_scalar_mul(out=sb1[:], in0=bias[:, 4:8], scalar1=SCALE)
+
         nb2 = const.tile([P, 4], F32, name="nb2")
         nc.vector.tensor_scalar_mul(out=nb2[:], in0=b2raw[:], scalar1=-1.0)
-        bh_bc = bias[:, 0:4].unsqueeze(1).to_broadcast([P, P, 4])
 
         w1c = const.tile([P, 512], U32, name="w1c", align_bytes=64)
         w1s = const.tile([P, 512], U8, name="w1s", align_bytes=64)
@@ -148,10 +157,9 @@ def tile_decoder_t_kernel(tc, digits, styles, images, W_h, b_h, W1, b1, W2, b2, 
             )
 
         def u0_a(t):
-            c = t // CH
             ct = psd.tile([P, 512], BF16, name="ct", tag="sd")
             for s in range(4):
-                nc.tensor.transpose(ct[:, s * P:(s + 1) * P], cat[c][:, (t % CH) * 4 + s, :], idb[:])
+                nc.tensor.transpose(ct[:, s * P:(s + 1) * P], cat[t][:, s, :], idb[:])
             catT[t] = work.tile([P, 512], BF16, name="catT", tag="catT", bufs=2)
             nc.vector.tensor_copy(out=catT[t][:], in_=ct[:])
             hg[t] = work.tile([P, 512, 4], BF16, name="hg", tag="hg", bufs=2, align_bytes=64)
@@ -195,8 +203,8 @@ def tile_decoder_t_kernel(tc, digits, styles, images, W_h, b_h, W1, b1, W2, b2, 
 
         def u0_q(t):
             flat = hg[t][:].rearrange("p w j -> p (w j)")
-            hq[t] = work.tile([P, 512], U32, name="hq", tag="hq", bufs=4, align_bytes=64)
-            hs[t] = work.tile([P, 512], U8, name="hs", tag="hs", bufs=4, align_bytes=64)
+            hq[t] = work.tile([P, 512], U32, name="hq", tag="hq", bufs=6, align_bytes=64)
+            hs[t] = work.tile([P, 512], U8, name="hs", tag="hs", bufs=6, align_bytes=64)
             nc.vector.quantize_mx(out=hq[t][:].bitcast(FP8X4), scales=hs[t][:], in_=flat)
 
         def u0_stream(tiles):
@@ -214,11 +222,12 @@ def tile_decoder_t_kernel(tc, digits, styles, images, W_h, b_h, W1, b1, W2, b2, 
             return pieces
 
         def mx_pass(c, i):
-            t = c * CH + (i % 16) // 4
+            half = 4 * CHUNKS[c]
+            t = sum(CHUNKS[:c]) + (i % half) // 4
             m = i % 4
             bank = pmm.tile([P, 512], F32, name="bank", tag="mm")
             pp[(c, i)] = bank
-            if i < 16:
+            if i < half:
                 wc, ws, ac, asc = w1c, w1s, hq[t], hs[t]
             else:
                 wc, ws, ac, asc = w2c, w2s, tq[t], ts[t]
@@ -233,21 +242,21 @@ def tile_decoder_t_kernel(tc, digits, styles, images, W_h, b_h, W1, b1, W2, b2, 
             )
 
         def act_er(c, i):
-            t = c * CH + i // 4
+            t = sum(CHUNKS[:c]) + i // 4
             m = i % 4
             if m == 0:
-                ee[t] = work.tile([P, 4, 512], F32, name="ee", tag="ee", bufs=2)
+                ee[t] = work.tile([P, 4, 512], F32, name="ee", tag="ee", bufs=3)
                 rr[t] = work.tile([P, 4, 512], BF16, name="rr", tag="rr", bufs=2)
             bank = pp[(c, i)]
             nc.scalar.activation(out=ee[t][:, m, :], in_=bank[:], func=ACTF.Exp, bias=b1e[:, m:m + 1], scale=1.0)
             nc.scalar.activation(out=rr[t][:, m, :], in_=bank[:], func=ACTF.Relu, bias=sb1[:, m:m + 1], scale=SCALE)
 
         def act_sig(c, i):
-            t = c * CH + i // 4
+            t = sum(CHUNKS[:c]) + i // 4
             m = i % 4
             if m == 0:
-                xx[t] = work.tile([P, 4, 512], F32, name="xx", tag="xx", bufs=4)
-            bank = pp[(c, 16 + i)]
+                xx[t] = work.tile([P, 4, 512], F32, name="xx", tag="xx", bufs=7)
+            bank = pp[(c, 4 * CHUNKS[c] + i)]
             nc.scalar.activation(out=xx[t][:, m, :], in_=bank[:], func=ACTF.Sigmoid, bias=nb2[:, m:m + 1], scale=-1.0)
 
         def c1(t):
@@ -264,45 +273,49 @@ def tile_decoder_t_kernel(tc, digits, styles, images, W_h, b_h, W1, b1, W2, b2, 
 
         def c1_q(t):
             tg = tgs[t]
-            tq[t] = work.tile([P, 512], U32, name="tq", tag="tq", bufs=4, align_bytes=64)
-            ts[t] = work.tile([P, 512], U8, name="ts", tag="ts", bufs=4, align_bytes=64)
+            tq[t] = work.tile([P, 512], U32, name="tq", tag="tq", bufs=7, align_bytes=64)
+            ts[t] = work.tile([P, 512], U8, name="ts", tag="ts", bufs=7, align_bytes=64)
             nc.vector.quantize_mx(
                 out=tq[t][:].bitcast(FP8X4), scales=ts[t][:], in_=tg[:].rearrange("p w j -> p (w j)")
             )
 
-        def ln(t):
-            aa[t] = work.tile([P, 4, 512], F32, name="aa", tag="aa", bufs=4)
-            bb[t] = work.tile([P, 4, 512], F32, name="bb", tag="bb", bufs=4)
-            xf = xx[t][:].rearrange("p m w -> p (m w)")
-            af = aa[t][:].rearrange("p m w -> p (m w)")
-            bf = bb[t][:].rearrange("p m w -> p (m w)")
-            nc.scalar.activation(out=bf, in_=xf, func=ACTF.Ln, bias=eps_t[:], scale=1.0)
-            nc.scalar.activation(out=af, in_=xf, func=ACTF.Ln, bias=ope_t[:], scale=-1.0)
+        def ln(t, x=slice(0, 4)):
+            if x.start == 0:
+                aa[t] = work.tile([P, 4, 512], F32, name="aa", tag="aa", bufs=4)
+                bb[t] = xx[t]
+            cut = [x.start * P, (x.start + x.stop) * P // 2, x.stop * P]
+            for w in (slice(cut[0], cut[1]), slice(cut[1], cut[2])):
+                nc.scalar.activation(out=aa[t][:, :, w], in_=xx[t][:, :, w], func=ACTF.Ln, bias=ope_t[:], scale=-1.0)
+            for w in (slice(cut[0], cut[1]), slice(cut[1], cut[2])):
+                nc.scalar.activation(out=bb[t][:, :, w], in_=xx[t][:, :, w], func=ACTF.Ln, bias=eps_t[:], scale=1.0)
 
-        def dd(t):
-            af = aa[t][:].rearrange("p m w -> p (m w)")
-            bf = bb[t][:].rearrange("p m w -> p (m w)")
-            nc.vector.scalar_tensor_tensor(out=af, in0=af, scalar=LN_EPS, in1=bf, op0=ALU.max, op1=ALU.subtract)
+        def dd(t, x=slice(0, 4)):
+            w = slice(x.start * P, x.stop * P)
+            nc.vector.scalar_tensor_tensor(
+                out=aa[t][:, :, w], in0=aa[t][:, :, w], scalar=LN_EPS, in1=bb[t][:, :, w], op0=ALU.max, op1=ALU.subtract
+            )
 
-        def tk(t, h):
-            imT = psd.tile([P, 4, P], F32, name="imT", tag="sd")
+        def tk(t, h, x=slice(0, 4)):
+            n = x.stop - x.start
+            imT = psd.tile([P, n, P], F32, name="imT", tag="sd")
             words = img[t][:].rearrange("p s x -> p (s x)").bitcast(F32)
-            for s in range(4):
-                nc.tensor.transpose(imT[:, s, :], words[:, s * 256 + h:(s + 1) * 256:2], idf[:])
+            for s in range(x.start, x.stop):
+                nc.tensor.transpose(imT[:, s - x.start, :], words[:, s * 256 + h:(s + 1) * 256:2], idf[:])
+            part = aa[t][:, 2 * h:2 * h + 2, x.start * P:x.stop * P]
             nc.vector.tensor_tensor(
-                out=aa[t][:, 2 * h:2 * h + 2, :],
-                in0=aa[t][:, 2 * h:2 * h + 2, :],
+                out=part,
+                in0=part,
                 in1=imT[:].rearrange("p s w -> p (s w)").bitcast(BF16).rearrange("p (x e) -> p e x", e=2),
                 op=ALU.mult,
             )
 
-        def ta(t, s):
-            if s == 0:
-                acc[t] = psd.tile([P, 4, P], F32, name="acc", tag="sd")
+        def ta(t, s, x=slice(0, 4)):
+            if s == x.start:
+                acc[(t, s)] = psd.tile([P, x.stop - x.start, P], F32, name="acc", tag="sd")
             terms = [bb[t][:, m, :] for m in range(4)] + [aa[t][:, m, :] for m in range(4)]
             for i in range(8):
                 nc.tensor.matmul(
-                    out=acc[t][:, s, :],
+                    out=acc[(t, x.start)][:, s - x.start, :],
                     lhsT=terms[i][:, s * P:(s + 1) * P],
                     rhs=idf[:],
                     is_transpose=True,
@@ -310,18 +323,19 @@ def tile_decoder_t_kernel(tc, digits, styles, images, W_h, b_h, W1, b1, W2, b2, 
                     stop=(i == 7),
                 )
 
-        def tr(t):
+        def tr(t, x=slice(0, 4)):
+            a = 4 * t + x.start
+            z = 4 * t + x.stop
             nc.vector.tensor_reduce(
-                out=out_sb[:, 4 * t:4 * t + 4, :].rearrange("p s g -> p (s g)"),
-                in_=acc[t][:].rearrange("p s (g r) -> p (s g) r", r=4),
+                out=out_sb[:, a:z, :].rearrange("p s g -> p (s g)"),
+                in_=acc[(t, x.start)][:].rearrange("p s (g r) -> p (s g) r", r=4),
                 axis=AX.X,
                 op=ALU.add,
                 negate=True,
             )
-            if t % CH == CH - 1:
-                c = t // CH
-                chunk = out_sb[:, 16 * c:16 * c + 16, :]
-                nc.sync.dma_start(out=outv[:, 16 * c:16 * c + 16, :], in_=chunk)
+            if z % 16 == 0 or t == NT - 1:
+                a = a if t == NT - 1 and x.start > 0 else 16 * (a // 16)
+                nc.sync.dma_start(out=outv[:, a:z, :], in_=out_sb[:, a:z, :])
 
         def more_img(t):
             if t + IB < NT:
@@ -337,31 +351,52 @@ def tile_decoder_t_kernel(tc, digits, styles, images, W_h, b_h, W1, b1, W2, b2, 
             pieces.append(lambda: tr(t))
             return pieces
 
+        halves = [slice(x, x + 2) for x in range(0, 4, 2)]
+
+        def last_pieces(x):
+            t = NT - 1
+            pieces = [lambda: dd(t, x), lambda: tk(t, 0, x), lambda: tk(t, 1, x)]
+            pieces = pieces + [(lambda s: (lambda: ta(t, s, x)))(s) for s in range(x.start, x.stop)]
+            return pieces + [lambda: tr(t, x)]
+
         def run(pieces):
             for f in pieces:
                 f()
 
+        passes = [(c, i) for c in range(len(CHUNKS)) for i in range(8 * CHUNKS[c])]
+        start = [sum(CHUNKS[:c]) for c in range(len(CHUNKS))]
+
+        def pump(limit):
+            while len(pp) < min(limit, len(passes)):
+                c, i = passes[len(pp)]
+                t = start[c] + (i % (4 * CHUNKS[c])) // 4
+                if t not in (hq if i < 4 * CHUNKS[c] else tq):
+                    return
+                mx_pass(c, i)
+
         run(u0_stream([0])[0:5])
+        biases()
         u0_a(1)
         quant_w1()
         u0_c(0)
         u0_q(0)
-        for i in range(LA):
-            mx_pass(0, i)
-        first = u0_stream([1, 2, 3])[1:]
+        pump(LA)
+        first = u0_stream(list(range(1, CHUNKS[0])))[1:]
         run(first[0:8])
         quant_w2()
         side = first[8:]
-        for c in range(NCH):
-            b = c * CH
-            n = b + CH
-            last = c == NCH - 1
+        done = 0
+        for c, n in enumerate(CHUNKS):
+            b = start[c]
+            last = b + n == NT
             if not last:
                 ld_cat(c + 1)
             used = 0
-            for i in range(16):
+            for i in range(4 * n):
+                pump(done + 1)
                 act_er(c, i)
-                mx_pass(c, i + LA)
+                done += 1
+                pump(done + LA)
                 for z in range(2):
                     if used < len(side):
                         side[used]()
@@ -373,35 +408,61 @@ def tile_decoder_t_kernel(tc, digits, styles, images, W_h, b_h, W1, b1, W2, b2, 
             side = side[used:]
             nxt = []
             if not last:
-                nxt = u0_stream([n, n + 1, n + 2, n + 3])
-            side = side + nxt[0:16]
+                nxt = u0_stream(list(range(b + n, b + n + CHUNKS[c + 1])))
+            early = min(len(nxt), max(16, 4 * n - len(side) - 3))
+            side = side + nxt[0:early]
             used = 0
-            for i in range(16):
+            quant_last = min(4, 4 * n - 9)
+            if quant_last < 0:
+                c1_q(b + n - 1)
+            for i in range(4 * n):
+                pump(done + 1)
                 act_sig(c, i)
-                if 16 + i + LA < 32:
-                    mx_pass(c, 16 + i + LA)
-                if i >= 3 and used < len(side):
-                    side[used]()
-                    used += 1
-                if i == 4:
-                    c1_q(b + 3)
+                done += 1
+                pump(done + LA)
+                if i >= 3:
+                    for z in range(1):
+                        if used < len(side):
+                            side[used]()
+                            used += 1
+                if i == quant_last:
+                    c1_q(b + n - 1)
             run(side[used:])
-            if not last:
-                for i in range(LA):
-                    mx_pass(c + 1, i)
-            ln(b)
-            run(nxt[16:22])
-            ln(b + 1)
-            run(nxt[22:])
-            run(tk_pieces(b))
-            ln(b + 2)
-            run(tk_pieces(b + 1))
-            ln(b + 3)
+            pump(done + LA)
+            rest = nxt[early:]
+            groups = min(n, max(2, n - 2))
+            for k in range(n):
+                if b + k == NT - 1:
+                    for x in halves:
+                        ln(b + k, x)
+                else:
+                    ln(b + k)
+                if k < groups:
+                    run(rest[len(rest) * k // groups:len(rest) * (k + 1) // groups])
+                if 1 <= k and k - 1 < n - 5 - 1:
+                    run(tk_pieces(b + k - 1))
             if last:
-                side = ta_pieces(b) + tk_pieces(b + 2) + ta_pieces(b + 1) + tk_pieces(b + 3)
+                side = []
+                for k in range(max(n - 5 - 1, 0), n):
+                    if k >= 2:
+                        side = side + ta_pieces(b + k - 2)
+                    if b + k < NT - 1:
+                        side = side + tk_pieces(b + k)
+                side = side + ta_pieces(NT - 2)
+                for x in halves:
+                    side = side + last_pieces(x)
             else:
-                run(ta_pieces(b))
-                run(tk_pieces(b + 2))
-                side = tk_pieces(b + 3) + ta_pieces(b + 1)
-            side = side + ta_pieces(b + 2) + ta_pieces(b + 3)
+                for k in range(0, n - 6):
+                    run(ta_pieces(b + k))
+                side = []
+                if n - 5 - 1 >= 0:
+                    run(tk_pieces(b + n - 5 - 1))
+                late = list(range(max(n - 6, 0), n))
+                for k in range(max(n - 5, 0), n):
+                    side = side + tk_pieces(b + k)
+                    if len(late) > n - k:
+                        side = side + ta_pieces(b + late[0])
+                        late = late[1:]
+                for k in late:
+                    side = side + ta_pieces(b + k)
         run(side)

@@ -21,7 +21,7 @@ NT = 16
 CHUNKS = [4, 6, 6]
 IB = 5
 LN_EPS = math.log(1e-9)
-LA = 4
+LA = 3
 FLOPS = 2 * 8192 * (128 * 512 + 2 * 512 * 512)
 
 ALPHA = 1.6732632423543772848170429916717

from contextlib import ExitStack
import math

import concourse.bass as bass
import concourse.mybir as mybir
import concourse.tile as tile
from concourse.masks import make_identity

F32 = mybir.dt.float32
BF16 = mybir.dt.bfloat16
U32 = mybir.dt.uint32
U8 = mybir.dt.uint8
FP8X4 = mybir.dt.float8_e4m3fn_x4
ALU = mybir.AluOpType
ACTF = mybir.ActivationFunctionType
AX = mybir.AxisListType

P = 128
NB = 64
NT = 16
CHUNKS = [4, 6, 6]
IB = 5
LN_EPS = math.log(1e-9)
LA = 3
FLOPS = 2 * 8192 * (128 * 512 + 2 * 512 * 512)

ALPHA = 1.6732632423543772848170429916717
SCALE = 1.0507009873554804934193349852946
SA = SCALE * ALPHA
LN_SA = math.log(SA)
EPS = 1e-9


def tile_decoder_t_kernel(tc, digits, styles, images, W_h, b_h, W1, b1, W2, b2, out):
    nc = tc.nc
    dig = digits.rearrange("s b d -> (s b) d").rearrange("(p n) d -> p n d", n=NB)
    sty = styles.rearrange("s b d -> (s b) d").rearrange("(p n) d -> p n d", n=NB)
    imgv = images.rearrange("s b c h w -> (s b) (c h w)").rearrange("(p n) x -> p n x", n=NB)
    outv = out.rearrange("s b c h -> (s b) (c h)").rearrange("(p n) g -> p n g", n=NB)

    with ExitStack() as ctx:
        ctx.enter_context(tc.manual_schedule(engines={mybir.EngineType.Activation}))
        const = ctx.enter_context(tc.tile_pool(name="const", bufs=1))
        work = ctx.enter_context(tc.tile_pool(name="work", bufs=2))
        pmm = ctx.enter_context(tc.psum_pool(name="pmm", bufs=LA))
        psd = ctx.enter_context(tc.psum_pool(name="psd", bufs=8 - LA))

        cat = {}
        catT = {}
        hg = {}
        hq = {}
        hs = {}
        ee = {}
        rr = {}
        tq = {}
        ts = {}
        xx = {}
        aa = {}
        bb = {}
        img = {}
        pp = {}
        tgs = {}
        acc = {}

        idb = const.tile([P, P], BF16, name="idb")
        idf = const.tile([P, P], F32, name="idf")
        make_identity(nc, idb[:])
        make_identity(nc, idf[:])
        brow = const.tile([P, P], BF16, name="brow")
        nc.vector.memset(brow[:], 0.0)
        brow2 = const.tile([P, P], BF16, name="brow2")
        nc.vector.memset(brow2[:], 0.0)
        sel = const.tile([P, 4, P], BF16, name="sel")
        nc.vector.tensor_copy(out=sel[:], in_=idb[:, 0:4].unsqueeze(2).to_broadcast([P, 4, P]))
        eps_t = const.tile([P, 1], F32, name="eps_t")
        ope_t = const.tile([P, 1], F32, name="ope_t")
        nc.vector.memset(eps_t[:], EPS)
        nc.vector.tensor_scalar_add(out=ope_t[:], in0=eps_t[:], scalar1=1.0)

        exp_t = const.tile([P, 1], F32, name="exp_t")
        nc.scalar.activation(out=exp_t[:], in_=eps_t[:], func=ACTF.Exp)

        def ld_cat(c):
            n = 4 * CHUNKS[c]
            x = 4 * sum(CHUNKS[:c])
            blocks = work.tile([P, n, P], BF16, name="cat", tag="cat", bufs=2)
            for t in range(CHUNKS[c]):
                cat[x // 4 + t] = blocks[:, 4 * t:4 * t + 4, :]
            if c > 0:
                ld_cat_blocks(blocks, x, 0, n)
            return blocks

        def ld_cat_blocks(blocks, x, u, v):
            nc.sync.dma_start(out=blocks[:, u:v, 0:32], in_=dig[:, x + u:x + v, :])
            nc.sync.dma_start(out=blocks[:, u:v, 32:128], in_=sty[:, x + u:x + v, :])

        def ld_img(t):
            img[t] = work.tile([P, 4, 512], BF16, name="img", tag="img", bufs=IB)
            nc.sync.dma_start(out=img[t][:], in_=imgv[:, 4 * t:4 * t + 4, :])

        first_blocks = ld_cat(0)
        ld_cat_blocks(first_blocks, 0, 0, 4)
        wh = const.tile([P, 512], BF16, name="wh")
        nc.sync.dma_start(out=wh[:], in_=W_h)
        nc.sync.dma_start(out=brow[0:4, :], in_=b_h.rearrange("(j c) -> j c", j=4))
        nc.sync.dma_start(out=brow[4:8, :], in_=b1.rearrange("(j c) -> j c", j=4))
        nc.sync.dma_start(out=brow2[0:4, :], in_=b_h.rearrange("(j c) -> j c", j=4))
        b2raw = const.tile([P, 4], BF16, name="b2raw")
        nc.sync.dma_start(out=b2raw[:], in_=b2.rearrange("(q m) -> q m", m=4))
        raw1 = work.tile([P, 4, 512], BF16, name="raw1", tag="raw", bufs=2)
        nc.sync.dma_start(out=raw1[:], in_=W1.rearrange("(j p) n -> p j n", p=P))
        ld_cat_blocks(first_blocks, 0, 4, 4 * CHUNKS[0])
        raw2 = work.tile([P, 4, 512], BF16, name="raw2", tag="raw", bufs=2)
        nc.sync.dma_start(out=raw2[:], in_=W2.rearrange("(j p) n -> p j n", p=P))
        for t in range(IB):
            ld_img(t)

        bias = const.tile([P, 8], F32, name="bias")
        b1e = const.tile([P, 4], F32, name="b1e")
        sb1 = const.tile([P, 4], F32, name="sb1")
        bh_bc = bias[:, 0:4].unsqueeze(1).to_broadcast([P, P, 4])

        def biases():
            pb = psd.tile([P, P], BF16, name="pb", tag="sd")
            nc.tensor.transpose(pb[:], brow[:], idb[:])
            nc.vector.tensor_copy(out=bias[:], in_=pb[:, 0:8])
            nc.vector.tensor_scalar_add(out=b1e[:], in0=bias[:, 4:8], scalar1=LN_SA)
            nc.vector.tensor_scalar_mul(out=sb1[:], in0=bias[:, 4:8], scalar1=SCALE)

        nb2 = const.tile([P, 4], F32, name="nb2")
        nc.vector.tensor_scalar_mul(out=nb2[:], in0=b2raw[:], scalar1=-1.0)

        w1c = const.tile([P, 512], U32, name="w1c", align_bytes=64)
        w1s = const.tile([P, 512], U8, name="w1s", align_bytes=64)
        w2c = const.tile([P, 512], U32, name="w2c", align_bytes=64)
        w2s = const.tile([P, 512], U8, name="w2s", align_bytes=64)
        out_sb = const.tile([P, NB, 32], F32, name="out_sb")

        grp1 = work.tile([P, 512, 4], BF16, name="grp1", tag="grp", bufs=2, align_bytes=64)
        nc.scalar.copy(
            out=grp1[:].rearrange("p (c i) j -> p c j i", i=4),
            in_=raw1[:].rearrange("p j (c i) -> p c j i", i=4),
        )
        grp2 = work.tile([P, 512, 4], BF16, name="grp2", tag="grp", bufs=2, align_bytes=64)
        src2 = raw2[:].rearrange("p j (q m) -> p m q j", m=4)
        for m in range(4):
            nc.scalar.copy(out=grp2[:, m * P:(m + 1) * P, :], in_=src2[:, m])

        def quant_w1():
            nc.vector.quantize_mx(
                out=w1c[:].bitcast(FP8X4), scales=w1s[:], in_=grp1[:].rearrange("p n j -> p (n j)")
            )

        def quant_w2():
            nc.vector.quantize_mx(
                out=w2c[:].bitcast(FP8X4), scales=w2s[:], in_=grp2[:].rearrange("p n j -> p (n j)")
            )

        def u0_a(t):
            ct = psd.tile([P, 512], BF16, name="ct", tag="sd")
            for s in range(4):
                nc.tensor.transpose(ct[:, s * P:(s + 1) * P], cat[t][:, s, :], idb[:])
            catT[t] = work.tile([P, 512], BF16, name="catT", tag="catT", bufs=2)
            nc.vector.tensor_copy(out=catT[t][:], in_=ct[:])
            hg[t] = work.tile([P, 512, 4], BF16, name="hg", tag="hg", bufs=2, align_bytes=64)

        def u0_b(t, s):
            p0 = psd.tile([P, 4, P], F32, name="p0", tag="sd")
            biased = t in range(8)
            if biased:
                nc.tensor.matmul(
                    out=p0[:].rearrange("p j w -> p (j w)"),
                    lhsT=brow2[:],
                    rhs=sel[:].rearrange("p j w -> p (j w)"),
                    start=True,
                    stop=False,
                )
            for j in range(4):
                nc.tensor.matmul(
                    out=p0[:, j, :],
                    lhsT=wh[:, j * P:(j + 1) * P],
                    rhs=catT[t][:, s * P:(s + 1) * P],
                    start=not biased,
                    stop=not biased or j == 3,
                )
            if biased:
                nc.vector.tensor_scalar_max(
                    out=hg[t][:, s * P:(s + 1) * P, :], in0=p0[:].rearrange("p j w -> p w j"), scalar1=0.0
                )
                return
            nc.vector.tensor_tensor(
                out=hg[t][:, s * P:(s + 1) * P, :],
                in0=p0[:].rearrange("p j w -> p w j"),
                in1=bh_bc,
                op=ALU.add,
            )

        def u0_c(t):
            if t in range(8):
                return
            flat = hg[t][:].rearrange("p w j -> p (w j)")
            nc.vector.tensor_scalar_max(out=flat, in0=flat, scalar1=0.0)

        def u0_q(t):
            flat = hg[t][:].rearrange("p w j -> p (w j)")
            hq[t] = work.tile([P, 512], U32, name="hq", tag="hq", bufs=6, align_bytes=64)
            hs[t] = work.tile([P, 512], U8, name="hs", tag="hs", bufs=6, align_bytes=64)
            nc.vector.quantize_mx(out=hq[t][:].bitcast(FP8X4), scales=hs[t][:], in_=flat)

        def u0_stream(tiles):
            pieces = [(lambda t: (lambda: u0_a(t)))(tiles[0])]
            for i in range(len(tiles)):
                t = tiles[i]
                for s in range(4):
                    if s == 2 and i + 1 < len(tiles):
                        pieces.append((lambda t: (lambda: u0_a(t)))(tiles[i + 1]))
                    pieces.append((lambda t, s: (lambda: u0_b(t, s)))(t, s))
                    if s == 0 and i > 0:
                        pieces.append((lambda t: (lambda: u0_q(t)))(tiles[i - 1]))
                pieces.append((lambda t: (lambda: u0_c(t)))(t))
            pieces.append((lambda t: (lambda: u0_q(t)))(tiles[len(tiles) - 1]))
            return pieces

        def mx_pass(c, i):
            half = 4 * CHUNKS[c]
            t = sum(CHUNKS[:c]) + (i % half) // 4
            m = i % 4
            bank = pmm.tile([P, 512], F32, name="bank", tag="mm")
            pp[(c, i)] = bank
            if i < half:
                wc, ws, ac, asc = w1c, w1s, hq[t], hs[t]
            else:
                wc, ws, ac, asc = w2c, w2s, tq[t], ts[t]
            nc.tensor.matmul_mx(
                out=bank[:],
                lhsT=wc[:, m * P:(m + 1) * P].bitcast(FP8X4),
                lhsT_scale=ws[:, m * P:(m + 1) * P],
                rhs=ac[:].bitcast(FP8X4),
                rhs_scale=asc[:],
                start=True,
                stop=True,
            )

        def act_er(c, i):
            t = sum(CHUNKS[:c]) + i // 4
            m = i % 4
            if m == 0:
                ee[t] = work.tile([P, 4, 512], F32, name="ee", tag="ee", bufs=3)
                rr[t] = work.tile([P, 4, 512], BF16, name="rr", tag="rr", bufs=2)
            bank = pp[(c, i)]
            nc.scalar.activation(out=ee[t][:, m, :], in_=bank[:], func=ACTF.Exp, bias=b1e[:, m:m + 1], scale=1.0)
            nc.scalar.activation(out=rr[t][:, m, :], in_=bank[:], func=ACTF.Relu, bias=sb1[:, m:m + 1], scale=SCALE)

        def act_sig(c, i):
            t = sum(CHUNKS[:c]) + i // 4
            m = i % 4
            if m == 0:
                xx[t] = work.tile([P, 4, 512], F32, name="xx", tag="xx", bufs=7)
            bank = pp[(c, 4 * CHUNKS[c] + i)]
            nc.scalar.activation(out=xx[t][:, m, :], in_=bank[:], func=ACTF.Sigmoid, bias=nb2[:, m:m + 1], scale=-1.0)

        def c1(t):
            tg = work.tile([P, 512, 4], BF16, name="tg", tag="tg", bufs=2, align_bytes=64)
            nc.vector.scalar_tensor_tensor(
                out=tg[:],
                in0=ee[t][:].rearrange("p j w -> p w j"),
                scalar=SA,
                in1=rr[t][:].rearrange("p j w -> p w j"),
                op0=ALU.subtract,
                op1=ALU.min,
            )
            tgs[t] = tg

        def c1_q(t):
            tg = tgs[t]
            tq[t] = work.tile([P, 512], U32, name="tq", tag="tq", bufs=7, align_bytes=64)
            ts[t] = work.tile([P, 512], U8, name="ts", tag="ts", bufs=7, align_bytes=64)
            nc.vector.quantize_mx(
                out=tq[t][:].bitcast(FP8X4), scales=ts[t][:], in_=tg[:].rearrange("p w j -> p (w j)")
            )

        def ln(t, x=slice(0, 4)):
            if x.start == 0:
                aa[t] = work.tile([P, 4, 512], F32, name="aa", tag="aa", bufs=4)
                bb[t] = xx[t]
            cut = [x.start * P, (x.start + x.stop) * P // 2, x.stop * P]
            for w in (slice(cut[0], cut[1]), slice(cut[1], cut[2])):
                nc.scalar.activation(out=aa[t][:, :, w], in_=xx[t][:, :, w], func=ACTF.Ln, bias=ope_t[:], scale=-1.0)
            for w in (slice(cut[0], cut[1]), slice(cut[1], cut[2])):
                nc.scalar.activation(out=bb[t][:, :, w], in_=xx[t][:, :, w], func=ACTF.Ln, bias=eps_t[:], scale=1.0)

        def dd(t, x=slice(0, 4)):
            w = slice(x.start * P, x.stop * P)
            nc.vector.scalar_tensor_tensor(
                out=aa[t][:, :, w], in0=aa[t][:, :, w], scalar=LN_EPS, in1=bb[t][:, :, w], op0=ALU.max, op1=ALU.subtract
            )

        def tk(t, h, x=slice(0, 4)):
            n = x.stop - x.start
            imT = psd.tile([P, n, P], F32, name="imT", tag="sd")
            words = img[t][:].rearrange("p s x -> p (s x)").bitcast(F32)
            for s in range(x.start, x.stop):
                nc.tensor.transpose(imT[:, s - x.start, :], words[:, s * 256 + h:(s + 1) * 256:2], idf[:])
            part = aa[t][:, 2 * h:2 * h + 2, x.start * P:x.stop * P]
            nc.vector.tensor_tensor(
                out=part,
                in0=part,
                in1=imT[:].rearrange("p s w -> p (s w)").bitcast(BF16).rearrange("p (x e) -> p e x", e=2),
                op=ALU.mult,
            )

        def ta(t, s, x=slice(0, 4)):
            if s == x.start:
                acc[(t, s)] = psd.tile([P, x.stop - x.start, P], F32, name="acc", tag="sd")
            terms = [bb[t][:, m, :] for m in range(4)] + [aa[t][:, m, :] for m in range(4)]
            for i in range(8):
                nc.tensor.matmul(
                    out=acc[(t, x.start)][:, s - x.start, :],
                    lhsT=terms[i][:, s * P:(s + 1) * P],
                    rhs=idf[:],
                    is_transpose=True,
                    start=(i == 0),
                    stop=(i == 7),
                )

        def tr(t, x=slice(0, 4)):
            a = 4 * t + x.start
            z = 4 * t + x.stop
            nc.vector.tensor_reduce(
                out=out_sb[:, a:z, :].rearrange("p s g -> p (s g)"),
                in_=acc[(t, x.start)][:].rearrange("p s (g r) -> p (s g) r", r=4),
                axis=AX.X,
                op=ALU.add,
                negate=True,
            )
            if z % 16 == 0 or t == NT - 1:
                a = a if t == NT - 1 and x.start > 0 else 16 * (a // 16)
                nc.sync.dma_start(out=outv[:, a:z, :], in_=out_sb[:, a:z, :])

        def more_img(t):
            if t + IB < NT:
                ld_img(t + IB)

        def tk_pieces(t):
            return [lambda: dd(t)] + [(lambda h: (lambda: tk(t, h)))(h) for h in range(2)] + [lambda: more_img(t)]

        def ta_pieces(t):
            pieces = []
            for s in range(4):
                pieces.append((lambda s: (lambda: ta(t, s)))(s))
            pieces.append(lambda: tr(t))
            return pieces

        halves = [slice(x, x + 2) for x in range(0, 4, 2)]

        def last_pieces(x):
            t = NT - 1
            pieces = [lambda: dd(t, x), lambda: tk(t, 0, x), lambda: tk(t, 1, x)]
            pieces = pieces + [(lambda s: (lambda: ta(t, s, x)))(s) for s in range(x.start, x.stop)]
            return pieces + [lambda: tr(t, x)]

        def run(pieces):
            for f in pieces:
                f()

        passes = [(c, i) for c in range(len(CHUNKS)) for i in range(8 * CHUNKS[c])]
        start = [sum(CHUNKS[:c]) for c in range(len(CHUNKS))]

        def pump(limit):
            while len(pp) < min(limit, len(passes)):
                c, i = passes[len(pp)]
                t = start[c] + (i % (4 * CHUNKS[c])) // 4
                if t not in (hq if i < 4 * CHUNKS[c] else tq):
                    return
                mx_pass(c, i)

        run(u0_stream([0])[0:5])
        biases()
        u0_a(1)
        quant_w1()
        u0_c(0)
        u0_q(0)
        pump(LA)
        first = u0_stream(list(range(1, CHUNKS[0])))[1:]
        run(first[0:8])
        quant_w2()
        side = first[8:]
        done = 0
        for c, n in enumerate(CHUNKS):
            b = start[c]
            last = b + n == NT
            if not last:
                ld_cat(c + 1)
            used = 0
            for i in range(4 * n):
                pump(done + 1)
                act_er(c, i)
                done += 1
                pump(done + LA)
                for z in range(2):
                    if used < len(side):
                        side[used]()
                        used += 1
                if i % 4 == 0 and i > 0:
                    c1_q(b + i // 4 - 1)
                if i % 4 == 3:
                    c1(b + i // 4)
            side = side[used:]
            nxt = []
            if not last:
                nxt = u0_stream(list(range(b + n, b + n + CHUNKS[c + 1])))
            early = min(len(nxt), max(16, 4 * n - len(side) - 3))
            side = side + nxt[0:early]
            used = 0
            quant_last = min(4, 4 * n - 9)
            if quant_last < 0:
                c1_q(b + n - 1)
            for i in range(4 * n):
                pump(done + 1)
                act_sig(c, i)
                done += 1
                pump(done + LA)
                if i >= 3:
                    for z in range(1):
                        if used < len(side):
                            side[used]()
                            used += 1
                if i == quant_last:
                    c1_q(b + n - 1)
            run(side[used:])
            pump(done + LA)
            rest = nxt[early:]
            groups = min(n, max(2, n - 2))
            for k in range(n):
                if b + k == NT - 1:
                    for x in halves:
                        ln(b + k, x)
                else:
                    ln(b + k)
                if k < groups:
                    run(rest[len(rest) * k // groups:len(rest) * (k + 1) // groups])
                if 1 <= k and k - 1 < n - 5 - 1:
                    run(tk_pieces(b + k - 1))
            if last:
                side = []
                for k in range(max(n - 5 - 1, 0), n):
                    if k >= 2:
                        side = side + ta_pieces(b + k - 2)
                    if b + k < NT - 1:
                        side = side + tk_pieces(b + k)
                side = side + ta_pieces(NT - 2)
                for x in halves:
                    side = side + last_pieces(x)
            else:
                for k in range(0, n - 6):
                    run(ta_pieces(b + k))
                side = []
                if n - 5 - 1 >= 0:
                    run(tk_pieces(b + n - 5 - 1))
                late = list(range(max(n - 6, 0), n))
                for k in range(max(n - 5, 0), n):
                    side = side + tk_pieces(b + k)
                    if len(late) > n - k:
                        side = side + ta_pieces(b + late[0])
                        late = late[1:]
                for k in late:
                    side = side + ta_pieces(b + k)
        run(side)
